import numpy as np
import ml_dtypes


def mxq(x, axis, fmt="e4m3"):
    dtype, down = {"e4m3": (ml_dtypes.float8_e4m3fn, 7), "e5m2": (ml_dtypes.float8_e5m2, 14)}[fmt]
    v = np.moveaxis(np.asarray(x, np.float32).astype(ml_dtypes.bfloat16).astype(np.float64), axis, -1)
    blocks = v.reshape(v.shape[:-1] + (-1, 32))
    amax = np.abs(blocks).max(-1, keepdims=True)
    byte = np.maximum(np.where(amax > 0, np.frexp(amax)[1] - 1 + 127, 0) - down, 1)
    scale = np.exp2(byte - 127.0)
    codes = (blocks / scale).astype(np.float32).astype(dtype).astype(np.float64)
    return np.moveaxis((codes * scale).reshape(v.shape), -1, axis)


WIDE = False


def mx_kscale(k):
    if not WIDE:
        return np.ones(k)
    levels = np.array([10, -10, 5, -5, 0])
    a = np.random.permutation(np.resize(levels, k // 512 * 4)).reshape(k // 512, 4)
    idx = np.arange(k)
    return np.exp2(a[idx // 512, idx % 128 // 32])


BF16 = ml_dtypes.bfloat16


def bf(x):
    return np.asarray(x, np.float32).astype(BF16)


def f64(x):
    return np.asarray(x).astype(np.float64)


B, N, F, U, S = 2, 2048, 128, 128, 2
C = S * (F + U)


def sigmoid(v):
    return 1.0 / (1.0 + np.exp(-v))


def random_walk():
    a = np.random.uniform(size=(N, N))
    return a / a.sum(axis=1, keepdims=True) * np.sqrt(N)


def setup_inputs():
    s = mx_kscale(N)
    return {"inputs": bf((np.random.standard_normal((B, F, N)) * s).reshape(B, F * N)),
            "state": bf((np.random.standard_normal((B, U, N)) * s).reshape(B, U * N)),
            "support0": bf(random_walk() / s[None, :]),
            "support1": bf(random_walk() / s[None, :]),
            "r_kernel": bf(np.random.standard_normal((C, U)) / np.sqrt(C)),
            "u_kernel": bf(np.random.standard_normal((C, U)) / np.sqrt(C))}


def diffuse(xq, supq):
    return np.concatenate([(xq @ sq.T) for sq in supq], axis=1)


def reference(inputs, state, support0, support1, r_kernel, u_kernel):
    supq = (mxq(f64(support0), 1, "e4m3"), mxq(f64(support1), 1, "e4m3"))
    feats = f64(inputs).reshape(B, F, N)
    prev = f64(state).reshape(B, U, N)
    h = diffuse(mxq(feats, 2, "e4m3"), supq).transpose(0, 2, 1)
    st = diffuse(mxq(prev, 2, "e4m3"), supq).transpose(0, 2, 1)
    hsq = mxq(np.concatenate([h, st], axis=-1), 2, "e4m3")
    r = sigmoid(hsq @ mxq(f64(r_kernel), 0, "e4m3"))
    u = sigmoid(hsq @ mxq(f64(u_kernel), 0, "e4m3"))
    return r, u, h

@@ -1,0 +1,274 @@
+from contextlib import ExitStack
+
+import concourse.mybir as mybir
+from concourse.masks import make_identity
+
+F32 = mybir.dt.float32
+BF16 = mybir.dt.bfloat16
+U32 = mybir.dt.uint32
+U8 = mybir.dt.uint8
+FP8X4 = mybir.dt.float8_e4m3fn_x4
+SIGMOID = mybir.ActivationFunctionType.Sigmoid
+
+P = 128
+NODES = 2048
+NBLK = 16
+RAW_BUFS = 8
+FLOPS = 2 * 2 * 512 * NODES * NODES + 2 * 4096 * 512 * 256
+
+
+def tile_gcrnncell_pa_kernel(tc, inputs, state, support0, support1, r_kernel, u_kernel, out_0, out_1, out_2):
+    nc = tc.nc
+    with ExitStack() as ctx:
+        const = ctx.enter_context(tc.tile_pool(name="const", bufs=1))
+        xraw_pool = ctx.enter_context(tc.tile_pool(name="xraw", bufs=4))
+        raw_pool = ctx.enter_context(tc.tile_pool(name="raw", bufs=RAW_BUFS))
+        grp_pool = ctx.enter_context(tc.tile_pool(name="grp", bufs=2))
+        code_pool = ctx.enter_context(tc.tile_pool(name="code", bufs=3))
+        hs_pool = ctx.enter_context(tc.tile_pool(name="hs", bufs=2))
+        out_pool = ctx.enter_context(tc.tile_pool(name="outs", bufs=3))
+        ps_t = ctx.enter_context(tc.psum_pool(name="pst", bufs=4))
+        ps_g = ctx.enter_context(tc.psum_pool(name="psg", bufs=1))
+        ps_h = ctx.enter_context(tc.psum_pool(name="psh", bufs=2))
+        ps_o = ctx.enter_context(tc.psum_pool(name="pso", bufs=1))
+        ctx.enter_context(tc.manual_schedule())
+
+        sup_view = [s.rearrange("(p t) n -> p t n", t=NBLK) for s in (support0, support1)]
+        x_view = [inputs.rearrange("b (c n) -> b c n", n=NODES), state.rearrange("b (c n) -> b c n", n=NODES)]
+        r_view = out_0.rearrange("b (p t) u -> p b t u", t=NBLK)
+        u_view = out_1.rearrange("b (p t) u -> p b t u", t=NBLK)
+        h_view = out_2.rearrange("b (p t) f -> p b t f", t=NBLK)
+
+        ident = const.tile([P, P], F32, name="ident", tag="ident")
+        make_identity(nc, ident[:])
+        warm_in = const.tile([P, 1], F32, name="warm_in", tag="warm_in")
+        warm_out = const.tile([P, 1], F32, name="warm_out", tag="warm_out")
+        nc.vector.memset(warm_in[:], 0.0)
+        nc.scalar.activation(out=warm_out[:], in_=warm_in[:], func=SIGMOID)
+
+        raw = {}
+
+        def load_x(kind, b):
+            t = xraw_pool.tile([P, NODES], BF16, name="xraw", tag="xraw")
+            nc.sync.dma_start(out=t[:], in_=x_view[kind][b])
+            return t
+
+        def load_sup(k):
+            for i in range(2):
+                t = raw_pool.tile([P, NODES], BF16, name="raw%d" % i, tag="raw%d" % i)
+                nc.sync.dma_start(out=t[:], in_=sup_view[i][:, k, :])
+                raw[(k, i)] = t
+
+        def copy_on(which, out, in_):
+            if which == 0:
+                nc.vector.tensor_copy(out=out, in_=in_)
+            else:
+                nc.scalar.copy(out=out, in_=in_)
+
+        xr = {}
+        xr[(0, 0)] = load_x(0, 0)
+        xr[(0, 1)] = load_x(0, 1)
+        load_sup(0)
+        xr[(1, 0)] = load_x(1, 0)
+        xr[(1, 1)] = load_x(1, 1)
+        load_sup(1)
+        wraw = const.tile([P, 2, 4, P], BF16, name="wraw", tag="wraw")
+        nc.sync.dma_start(out=wraw[:, 0], in_=r_kernel.rearrange("(t p) u -> p t u", p=P))
+        nc.sync.dma_start(out=wraw[:, 1], in_=u_kernel.rearrange("(t p) u -> p t u", p=P))
+        for k in range(2, RAW_BUFS):
+            load_sup(k)
+
+        xcodes = []
+        xscales = []
+
+        def prepare_x(kind):
+            xg = const.tile([P, 4096], BF16, name="xg%d" % kind, tag="xg%d" % kind, align_bytes=64)
+            xc = const.tile([P, 1024], U32, name="xc%d" % kind, tag="xc%d" % kind, align_bytes=64)
+            xs = const.tile([P, 1024], U8, name="xs%d" % kind, tag="xs%d" % kind, align_bytes=64)
+            xg32 = xg[:].bitcast(F32).rearrange("p (g b c u) -> p g b c u", g=4, b=2, u=2)
+            for b in range(2):
+                words = xr[(kind, b)][:].bitcast(F32)
+                for gp in range(2):
+                    tp = ps_t.tile([P, 512], F32, name="tp", tag="tp")
+                    for gg in range(2):
+                        for u in range(2):
+                            col = 256 * (2 * gp + gg) + 128 * u
+                            dst = (2 * gg + u) * P
+                            nc.tensor.transpose(tp[:, dst:dst + P], words[:, col:col + P], ident[:])
+                    copy_on(gp, xg32[:, 2 * gp:2 * gp + 2, b, :, :], tp[:].rearrange("p (g u c) -> p g c u", g=2, u=2))
+            for half in range(2):
+                nc.vector.quantize_mx(
+                    out=xc[:, 512 * half:512 * half + 512].bitcast(FP8X4),
+                    scales=xs[:, 512 * half:512 * half + 512],
+                    in_=xg[:, 2048 * half:2048 * half + 2048],
+                )
+            xcodes.append(xc)
+            xscales.append(xs)
+
+        sup_codes = {}
+        state_of = {}
+
+        def transpose_bank(k, g, grouped):
+            tp = ps_t.tile([P, 512], F32, name="tp", tag="tp")
+            for i in range(2):
+                words = raw[(k, i)][:].bitcast(F32)
+                for u in range(2):
+                    col = 256 * g + 128 * u
+                    dst = (2 * i + u) * P
+                    nc.tensor.transpose(tp[:, dst:dst + P], words[:, col:col + P], ident[:])
+            copy_on(
+                g % 2,
+                grouped[:].bitcast(F32)[:, 512 * g:512 * g + 512].rearrange("p (i m u) -> p i m u", i=2, u=2),
+                tp[:].rearrange("p (i u m) -> p i m u", i=2, u=2),
+            )
+
+        def quantise_sup(k, grouped):
+            sc = code_pool.tile([P, 1024], U32, name="sc", tag="sc", align_bytes=64)
+            ss = code_pool.tile([P, 1024], U8, name="ss", tag="ss", align_bytes=64)
+            for half in range(2):
+                nc.vector.quantize_mx(
+                    out=sc[:, 512 * half:512 * half + 512].bitcast(FP8X4),
+                    scales=ss[:, 512 * half:512 * half + 512],
+                    in_=grouped[:, 2048 * half:2048 * half + 2048],
+                )
+            sup_codes[k] = (sc, ss)
+
+        def quantise_hs(k):
+            g2 = state_of[k]["g2"]
+            g2c = hs_pool.tile([P, 256], U32, name="g2c", tag="g2c", align_bytes=64)
+            g2s = hs_pool.tile([P, 256], U8, name="g2s", tag="g2s", align_bytes=64)
+            nc.vector.quantize_mx(out=g2c[:].bitcast(FP8X4), scales=g2s[:], in_=g2[:])
+            state_of[k]["g2c"] = g2c
+            state_of[k]["g2s"] = g2s
+
+        def plain_phase(k_h, k_t):
+            if k_h is not None:
+                st = state_of[k_h]
+                g2 = hs_pool.tile([P, 1024], BF16, name="g2", tag="g2", align_bytes=64)
+                st["g2"] = g2
+                for b in range(2):
+                    for i in range(2):
+                        nc.tensor.transpose(st["H"][b][:, i * P:(i + 1) * P], st["h32"][:, b, k_h % 2, i, :], ident[:])
+                    copy_on(
+                        b,
+                        g2[:, 512 * b:512 * b + 512].rearrange("p (m t) -> p m t", t=4),
+                        st["H"][b][:].rearrange("p (t m) -> p m t", t=4),
+                    )
+            if k_t is not None:
+                grouped = grp_pool.tile([P, 4096], BF16, name="grouped", tag="grouped", align_bytes=64)
+                transpose_bank(k_t, 0, grouped)
+                transpose_bank(k_t, 1, grouped)
+                if k_h is not None:
+                    quantise_hs(k_h)
+                transpose_bank(k_t, 2, grouped)
+                transpose_bank(k_t, 3, grouped)
+                quantise_sup(k_t, grouped)
+                if k_t + RAW_BUFS < NBLK:
+                    load_sup(k_t + RAW_BUFS)
+            elif k_h is not None:
+                quantise_hs(k_h)
+
+        pair_tiles = {}
+
+        def feats_passes(k):
+            sc, ss = sup_codes[k]
+            gb = ps_g.tile([P, 512], F32, name="gb", tag="gb")
+            for i in range(2):
+                for g in range(4):
+                    a = (2 * g + i) * P
+                    nc.tensor.matmul_mx(
+                        out=gb[:, 256 * i:256 * i + 256],
+                        lhsT=sc[:, a:a + P].bitcast(FP8X4),
+                        lhsT_scale=ss[:, a:a + P],
+                        rhs=xcodes[0][:, 256 * g:256 * g + 256].bitcast(FP8X4),
+                        rhs_scale=xscales[0][:, 256 * g:256 * g + 256],
+                        start=(g == 0),
+                        stop=(g == 3),
+                    )
+            if k % 2 == 0:
+                h32 = out_pool.tile([P, 2, 2, 2, P], F32, name="h32", tag="h32")
+                pair_tiles[("h", k // 2)] = h32
+            h32 = pair_tiles[("h", k // 2)]
+            nc.scalar.copy(out=h32[:, :, k % 2, :, :], in_=gb[:].rearrange("p (i b c) -> p b i c", i=2, b=2))
+            state_of[k] = {"h32": h32}
+
+        def prev_passes(k):
+            sc, ss = sup_codes[k]
+            banks = []
+            for b in range(2):
+                hb = ps_h.tile([P, 512], F32, name="hb", tag="hb")
+                for g in range(4):
+                    a = (2 * g + b) * P
+                    nc.tensor.matmul_mx(
+                        out=hb[:, 256:512],
+                        lhsT=xcodes[1][:, a:a + P].bitcast(FP8X4),
+                        lhsT_scale=xscales[1][:, a:a + P],
+                        rhs=sc[:, 256 * g:256 * g + 256].bitcast(FP8X4),
+                        rhs_scale=ss[:, 256 * g:256 * g + 256],
+                        start=(g == 0),
+                        stop=(g == 3),
+                    )
+                banks.append(hb)
+            state_of[k]["H"] = banks
+
+        def gate_passes(k):
+            st = state_of[k]
+            ob = ps_o.tile([P, 512], F32, name="ob", tag="ob")
+            for b in range(2):
+                nc.tensor.matmul_mx(
+                    out=ob[:, 256 * b:256 * b + 256],
+                    lhsT=st["g2c"][:, P * b:P * b + P].bitcast(FP8X4),
+                    lhsT_scale=st["g2s"][:, P * b:P * b + P],
+                    rhs=wc[:].bitcast(FP8X4),
+                    rhs_scale=ws[:],
+                    start=True,
+                    stop=True,
+                )
+            return ob
+
+        def gate_sigmoid(k, ob):
+            if k % 2 == 0:
+                ru = out_pool.tile([P, 2, 2, 2, P], F32, name="ru", tag="ru")
+                pair_tiles[("ru", k // 2)] = ru
+            ru = pair_tiles[("ru", k // 2)]
+            nc.scalar.activation(
+                out=ru[:, :, :, k % 2, :].rearrange("p r b u -> p b r u"),
+                in_=ob[:].rearrange("p (b r u) -> p b r u", b=2, r=2),
+                func=SIGMOID,
+            )
+
+        def store_h(q):
+            nc.sync.dma_start(
+                out=h_view[:, :, 2 * q:2 * q + 2, :],
+                in_=pair_tiles[("h", q)][:].rearrange("p b t i c -> p b t (i c)"),
+            )
+
+        def store_ru(q):
+            ru = pair_tiles[("ru", q)]
+            nc.sync.dma_start(out=r_view[:, :, 2 * q:2 * q + 2, :], in_=ru[:, 0])
+            nc.sync.dma_start(out=u_view[:, :, 2 * q:2 * q + 2, :], in_=ru[:, 1])
+
+        prepare_x(0)
+        plain_phase(None, 0)
+        prepare_x(1)
+
+        wg = const.tile([P, 2, P, 4], BF16, name="wg", tag="wg", align_bytes=64)
+        wc = const.tile([P, 256], U32, name="wc", tag="wc", align_bytes=64)
+        ws = const.tile([P, 256], U8, name="ws", tag="ws", align_bytes=64)
+
+        for it in range(NBLK + 1):
+            plain_phase(it - 1 if it >= 1 else None, it + 1 if it + 1 < NBLK else None)
+            if it == 0:
+                nc.vector.tensor_copy(out=wg[:], in_=wraw[:].rearrange("p r t u -> p r u t"))
+                nc.vector.quantize_mx(out=wc[:].bitcast(FP8X4), scales=ws[:], in_=wg[:].rearrange("p r u t -> p (r u t)"))
+            if it < NBLK:
+                feats_passes(it)
+            if it >= 1:
+                ob = gate_passes(it - 1)
+                gate_sigmoid(it - 1, ob)
+            if it < NBLK:
+                prev_passes(it)
+            if it < NBLK and it % 2 == 1:
+                store_h(it // 2)
+            if it >= 1 and (it - 1) % 2 == 1:
+                store_ru((it - 1) // 2)

@@ -122,16 +122,18 @@ def tile_gcrnncell_pa_kernel(tc, inputs, state, support0, support1, r_kernel, u_
                 tp[:].rearrange("p (i u m) -> p i m u", i=2, u=2),
             )
 
-        def quantise_sup(k, grouped):
+        def new_sup_codes(k):
             sc = code_pool.tile([P, 1024], U32, name="sc", tag="sc", align_bytes=64)
             ss = code_pool.tile([P, 1024], U8, name="ss", tag="ss", align_bytes=64)
-            for half in range(2):
-                nc.vector.quantize_mx(
-                    out=sc[:, 512 * half:512 * half + 512].bitcast(FP8X4),
-                    scales=ss[:, 512 * half:512 * half + 512],
-                    in_=grouped[:, 2048 * half:2048 * half + 2048],
-                )
             sup_codes[k] = (sc, ss)
+
+        def quantise_sup(k, grouped, half):
+            sc, ss = sup_codes[k]
+            nc.vector.quantize_mx(
+                out=sc[:, 512 * half:512 * half + 512].bitcast(FP8X4),
+                scales=ss[:, 512 * half:512 * half + 512],
+                in_=grouped[:, 2048 * half:2048 * half + 2048],
+            )
 
         def quantise_hs(k):
             g2 = state_of[k]["g2"]
@@ -141,31 +143,39 @@ def tile_gcrnncell_pa_kernel(tc, inputs, state, support0, support1, r_kernel, u_
             state_of[k]["g2c"] = g2c
             state_of[k]["g2s"] = g2s
 
-        def plain_phase(k_h, k_t):
-            if k_h is not None:
-                st = state_of[k_h]
+        def transpose_h(k, b):
+            st = state_of[k]
+            if b == 0:
                 g2 = hs_pool.tile([P, 1024], BF16, name="g2", tag="g2", align_bytes=64)
                 st["g2"] = g2
-                for b in range(2):
-                    for i in range(2):
-                        nc.tensor.transpose(st["H"][b][:, i * P:(i + 1) * P], st["h32"][:, b, k_h % 2, i, :], ident[:])
-                    copy_on(
-                        b,
-                        g2[:, 512 * b:512 * b + 512].rearrange("p (m t) -> p m t", t=4),
-                        st["H"][b][:].rearrange("p (t m) -> p m t", t=4),
-                    )
+            g2 = st["g2"]
+            for i in range(2):
+                nc.tensor.transpose(st["H"][b][:, i * P:(i + 1) * P], st["h32"][:, b, k % 2, i, :], ident[:])
+            copy_on(
+                b,
+                g2[:, 512 * b:512 * b + 512].rearrange("p (m t) -> p m t", t=4),
+                st["H"][b][:].rearrange("p (t m) -> p m t", t=4),
+            )
+
+        grouped_of = {}
+
+        def plain_half(k_h, k_t, half):
+            if k_h is not None:
+                transpose_h(k_h, half)
             if k_t is not None:
-                grouped = grp_pool.tile([P, 4096], BF16, name="grouped", tag="grouped", align_bytes=64)
-                transpose_bank(k_t, 0, grouped)
-                transpose_bank(k_t, 1, grouped)
-                if k_h is not None:
+                if half == 0:
+                    grouped = grp_pool.tile([P, 4096], BF16, name="grouped", tag="grouped", align_bytes=64)
+                    grouped_of[k_t] = grouped
+                    new_sup_codes(k_t)
+                grouped = grouped_of[k_t]
+                if half == 1 and k_h is not None:
                     quantise_hs(k_h)
-                transpose_bank(k_t, 2, grouped)
-                transpose_bank(k_t, 3, grouped)
-                quantise_sup(k_t, grouped)
-                if k_t + RAW_BUFS < NBLK:
+                transpose_bank(k_t, 2 * half, grouped)
+                transpose_bank(k_t, 2 * half + 1, grouped)
+                quantise_sup(k_t, grouped, half)
+                if half == 1 and k_t + RAW_BUFS < NBLK:
                     load_sup(k_t + RAW_BUFS)
-            elif k_h is not None:
+            elif half == 1 and k_h is not None:
                 quantise_hs(k_h)
 
         pair_tiles = {}
@@ -249,7 +259,8 @@ def tile_gcrnncell_pa_kernel(tc, inputs, state, support0, support1, r_kernel, u_
             nc.sync.dma_start(out=u_view[:, :, 2 * q:2 * q + 2, :], in_=ru[:, 1])
 
         prepare_x(0)
-        plain_phase(None, 0)
+        plain_half(None, 0, 0)
+        plain_half(None, 0, 1)
         prepare_x(1)
 
         wg = const.tile([P, 2, P, 4], BF16, name="wg", tag="wg", align_bytes=64)
@@ -257,17 +268,20 @@ def tile_gcrnncell_pa_kernel(tc, inputs, state, support0, support1, r_kernel, u_
         ws = const.tile([P, 256], U8, name="ws", tag="ws", align_bytes=64)
 
         for it in range(NBLK + 1):
-            plain_phase(it - 1 if it >= 1 else None, it + 1 if it + 1 < NBLK else None)
+            k_h = it - 1 if it >= 1 else None
+            k_t = it + 1 if it + 1 < NBLK else None
+            plain_half(k_h, k_t, 0)
+            if it < NBLK:
+                feats_passes(it)
+            plain_half(k_h, k_t, 1)
             if it == 0:
                 nc.vector.tensor_copy(out=wg[:], in_=wraw[:].rearrange("p r t u -> p r u t"))
                 nc.vector.quantize_mx(out=wc[:].bitcast(FP8X4), scales=ws[:], in_=wg[:].rearrange("p r u t -> p (r u t)"))
             if it < NBLK:
-                feats_passes(it)
+                prev_passes(it)
             if it >= 1:
                 ob = gate_passes(it - 1)
                 gate_sigmoid(it - 1, ob)
-            if it < NBLK:
-                prev_passes(it)
             if it < NBLK and it % 2 == 1:
                 store_h(it // 2)
             if it >= 1 and (it - 1) % 2 == 1:

@@ -14,6 +14,7 @@ P = 128
 NODES = 2048
 NBLK = 16
 RAW_BUFS = 8
+GROUPS = ((0,), (1,), (2, 3), (4, 5), (6, 7), (8, 9), (10, 11), (12, 13), (14,), (15,))
 FLOPS = 2 * 2 * 512 * NODES * NODES + 2 * 4096 * 512 * 256
 
 
@@ -21,16 +22,16 @@ def tile_gcrnncell_pa_kernel(tc, inputs, state, support0, support1, r_kernel, u_
     nc = tc.nc
     with ExitStack() as ctx:
         const = ctx.enter_context(tc.tile_pool(name="const", bufs=1))
-        xraw_pool = ctx.enter_context(tc.tile_pool(name="xraw", bufs=4))
+        xraw_pool = ctx.enter_context(tc.tile_pool(name="xraw", bufs=2))
         raw_pool = ctx.enter_context(tc.tile_pool(name="raw", bufs=RAW_BUFS))
-        grp_pool = ctx.enter_context(tc.tile_pool(name="grp", bufs=2))
-        code_pool = ctx.enter_context(tc.tile_pool(name="code", bufs=3))
-        hs_pool = ctx.enter_context(tc.tile_pool(name="hs", bufs=2))
-        out_pool = ctx.enter_context(tc.tile_pool(name="outs", bufs=3))
-        ps_t = ctx.enter_context(tc.psum_pool(name="pst", bufs=4))
-        ps_g = ctx.enter_context(tc.psum_pool(name="psg", bufs=1))
-        ps_h = ctx.enter_context(tc.psum_pool(name="psh", bufs=2))
-        ps_o = ctx.enter_context(tc.psum_pool(name="pso", bufs=1))
+        grp_pool = ctx.enter_context(tc.tile_pool(name="grp", bufs=4))
+        code_pool = ctx.enter_context(tc.tile_pool(name="code", bufs=7))
+        g2_pool = ctx.enter_context(tc.tile_pool(name="g2p", bufs=6))
+        g2c_pool = ctx.enter_context(tc.tile_pool(name="g2cp", bufs=4))
+        h_pool = ctx.enter_context(tc.tile_pool(name="hp", bufs=3))
+        ru_pool = ctx.enter_context(tc.tile_pool(name="rup", bufs=2))
+        ps_t = ctx.enter_context(tc.psum_pool(name="pst", bufs=5))
+        ps_m = ctx.enter_context(tc.psum_pool(name="psm", bufs=3))
         ctx.enter_context(tc.manual_schedule())
 
         sup_view = [s.rearrange("(p t) n -> p t n", t=NBLK) for s in (support0, support1)]
@@ -38,6 +39,11 @@ def tile_gcrnncell_pa_kernel(tc, inputs, state, support0, support1, r_kernel, u_
         r_view = out_0.rearrange("b (p t) u -> p b t u", t=NBLK)
         u_view = out_1.rearrange("b (p t) u -> p b t u", t=NBLK)
         h_view = out_2.rearrange("b (p t) f -> p b t f", t=NBLK)
+
+        group_of = {}
+        for gi, blocks in enumerate(GROUPS):
+            for pos, k in enumerate(blocks):
+                group_of[k] = (gi, pos)
 
         ident = const.tile([P, P], F32, name="ident", tag="ident")
         make_identity(nc, ident[:])
@@ -69,20 +75,12 @@ def tile_gcrnncell_pa_kernel(tc, inputs, state, support0, support1, r_kernel, u_
         xr[(0, 0)] = load_x(0, 0)
         xr[(0, 1)] = load_x(0, 1)
         load_sup(0)
-        xr[(1, 0)] = load_x(1, 0)
-        xr[(1, 1)] = load_x(1, 1)
-        load_sup(1)
-        wraw = const.tile([P, 2, 4, P], BF16, name="wraw", tag="wraw")
-        nc.sync.dma_start(out=wraw[:, 0], in_=r_kernel.rearrange("(t p) u -> p t u", p=P))
-        nc.sync.dma_start(out=wraw[:, 1], in_=u_kernel.rearrange("(t p) u -> p t u", p=P))
-        for k in range(2, RAW_BUFS):
-            load_sup(k)
 
         xcodes = []
         xscales = []
 
         def prepare_x(kind):
-            xg = const.tile([P, 4096], BF16, name="xg%d" % kind, tag="xg%d" % kind, align_bytes=64)
+            xg = grp_pool.tile([P, 4096], BF16, name="grouped", tag="grouped", align_bytes=64)
             xc = const.tile([P, 1024], U32, name="xc%d" % kind, tag="xc%d" % kind, align_bytes=64)
             xs = const.tile([P, 1024], U8, name="xs%d" % kind, tag="xs%d" % kind, align_bytes=64)
             xg32 = xg[:].bitcast(F32).rearrange("p (g b c u) -> p g b c u", g=4, b=2, u=2)
@@ -106,83 +104,48 @@ def tile_gcrnncell_pa_kernel(tc, inputs, state, support0, support1, r_kernel, u_
             xscales.append(xs)
 
         sup_codes = {}
-        state_of = {}
+        grouped_of = {}
+        g2_of = {}
+        g2q_of = {}
+        h_of = {}
+        ru_of = {}
 
-        def transpose_bank(k, g, grouped):
-            tp = ps_t.tile([P, 512], F32, name="tp", tag="tp")
-            for i in range(2):
-                words = raw[(k, i)][:].bitcast(F32)
-                for u in range(2):
-                    col = 256 * g + 128 * u
-                    dst = (2 * i + u) * P
-                    nc.tensor.transpose(tp[:, dst:dst + P], words[:, col:col + P], ident[:])
-            copy_on(
-                g % 2,
-                grouped[:].bitcast(F32)[:, 512 * g:512 * g + 512].rearrange("p (i m u) -> p i m u", i=2, u=2),
-                tp[:].rearrange("p (i u m) -> p i m u", i=2, u=2),
-            )
+        def transpose_sup(k, pos):
+            grouped = grp_pool.tile([P, 4096], BF16, name="grouped", tag="grouped", align_bytes=64)
+            grouped_of[k] = grouped
+            engines = (0, pos % 2, 0, 1)
+            for g in range(4):
+                tp = ps_t.tile([P, 512], F32, name="tp", tag="tp")
+                for i in range(2):
+                    words = raw[(k, i)][:].bitcast(F32)
+                    for u in range(2):
+                        col = 256 * g + 128 * u
+                        dst = (2 * i + u) * P
+                        nc.tensor.transpose(tp[:, dst:dst + P], words[:, col:col + P], ident[:])
+                copy_on(
+                    engines[g],
+                    grouped[:].bitcast(F32)[:, 512 * g:512 * g + 512].rearrange("p (i m u) -> p i m u", i=2, u=2),
+                    tp[:].rearrange("p (i u m) -> p i m u", i=2, u=2),
+                )
+            if k + RAW_BUFS < NBLK:
+                load_sup(k + RAW_BUFS)
 
-        def new_sup_codes(k):
+        def quantise_sup(k):
+            grouped = grouped_of[k]
             sc = code_pool.tile([P, 1024], U32, name="sc", tag="sc", align_bytes=64)
             ss = code_pool.tile([P, 1024], U8, name="ss", tag="ss", align_bytes=64)
+            for half in range(2):
+                nc.vector.quantize_mx(
+                    out=sc[:, 512 * half:512 * half + 512].bitcast(FP8X4),
+                    scales=ss[:, 512 * half:512 * half + 512],
+                    in_=grouped[:, 2048 * half:2048 * half + 2048],
+                )
             sup_codes[k] = (sc, ss)
 
-        def quantise_sup(k, grouped, half):
-            sc, ss = sup_codes[k]
-            nc.vector.quantize_mx(
-                out=sc[:, 512 * half:512 * half + 512].bitcast(FP8X4),
-                scales=ss[:, 512 * half:512 * half + 512],
-                in_=grouped[:, 2048 * half:2048 * half + 2048],
-            )
-
-        def quantise_hs(k):
-            g2 = state_of[k]["g2"]
-            g2c = hs_pool.tile([P, 256], U32, name="g2c", tag="g2c", align_bytes=64)
-            g2s = hs_pool.tile([P, 256], U8, name="g2s", tag="g2s", align_bytes=64)
-            nc.vector.quantize_mx(out=g2c[:].bitcast(FP8X4), scales=g2s[:], in_=g2[:])
-            state_of[k]["g2c"] = g2c
-            state_of[k]["g2s"] = g2s
-
-        def transpose_h(k, b):
-            st = state_of[k]
-            if b == 0:
-                g2 = hs_pool.tile([P, 1024], BF16, name="g2", tag="g2", align_bytes=64)
-                st["g2"] = g2
-            g2 = st["g2"]
-            for i in range(2):
-                nc.tensor.transpose(st["H"][b][:, i * P:(i + 1) * P], st["h32"][:, b, k % 2, i, :], ident[:])
-            copy_on(
-                b,
-                g2[:, 512 * b:512 * b + 512].rearrange("p (m t) -> p m t", t=4),
-                st["H"][b][:].rearrange("p (t m) -> p m t", t=4),
-            )
-
-        grouped_of = {}
-
-        def plain_half(k_h, k_t, half):
-            if k_h is not None:
-                transpose_h(k_h, half)
-            if k_t is not None:
-                if half == 0:
-                    grouped = grp_pool.tile([P, 4096], BF16, name="grouped", tag="grouped", align_bytes=64)
-                    grouped_of[k_t] = grouped
-                    new_sup_codes(k_t)
-                grouped = grouped_of[k_t]
-                if half == 1 and k_h is not None:
-                    quantise_hs(k_h)
-                transpose_bank(k_t, 2 * half, grouped)
-                transpose_bank(k_t, 2 * half + 1, grouped)
-                quantise_sup(k_t, grouped, half)
-                if half == 1 and k_t + RAW_BUFS < NBLK:
-                    load_sup(k_t + RAW_BUFS)
-            elif half == 1 and k_h is not None:
-                quantise_hs(k_h)
-
-        pair_tiles = {}
-
         def feats_passes(k):
+            gi, pos = group_of[k]
             sc, ss = sup_codes[k]
-            gb = ps_g.tile([P, 512], F32, name="gb", tag="gb")
+            gb = ps_m.tile([P, 512], F32, name="mx", tag="mx")
             for i in range(2):
                 for g in range(4):
                     a = (2 * g + i) * P
@@ -195,22 +158,19 @@ def tile_gcrnncell_pa_kernel(tc, inputs, state, support0, support1, r_kernel, u_
                         start=(g == 0),
                         stop=(g == 3),
                     )
-            if k % 2 == 0:
-                h32 = out_pool.tile([P, 2, 2, 2, P], F32, name="h32", tag="h32")
-                pair_tiles[("h", k // 2)] = h32
-            h32 = pair_tiles[("h", k // 2)]
-            nc.scalar.copy(out=h32[:, :, k % 2, :, :], in_=gb[:].rearrange("p (i b c) -> p b i c", i=2, b=2))
-            state_of[k] = {"h32": h32}
+            if pos == 0:
+                h32 = h_pool.tile([P, 2, len(GROUPS[gi]), 2, P], F32, name="h32", tag="h32")
+                h_of[gi] = h32
+            nc.scalar.copy(out=h_of[gi][:, :, pos, :, :], in_=gb[:].rearrange("p (i b c) -> p b i c", i=2, b=2))
 
         def prev_passes(k):
             sc, ss = sup_codes[k]
-            banks = []
+            sb = ps_m.tile([P, 512], F32, name="mx", tag="mx")
             for b in range(2):
-                hb = ps_h.tile([P, 512], F32, name="hb", tag="hb")
                 for g in range(4):
                     a = (2 * g + b) * P
                     nc.tensor.matmul_mx(
-                        out=hb[:, 256:512],
+                        out=sb[:, 256 * b:256 * b + 256],
                         lhsT=xcodes[1][:, a:a + P].bitcast(FP8X4),
                         lhsT_scale=xscales[1][:, a:a + P],
                         rhs=sc[:, 256 * g:256 * g + 256].bitcast(FP8X4),
@@ -218,71 +178,106 @@ def tile_gcrnncell_pa_kernel(tc, inputs, state, support0, support1, r_kernel, u_
                         start=(g == 0),
                         stop=(g == 3),
                     )
-                banks.append(hb)
-            state_of[k]["H"] = banks
+            g2 = g2_pool.tile([P, 1024], BF16, name="g2", tag="g2", align_bytes=64)
+            g2_of[k] = g2
+            nc.scalar.copy(
+                out=g2[:].rearrange("p (b m t) -> p b m t", b=2, t=4)[:, :, :, 2:4],
+                in_=sb[:].rearrange("p (b i m) -> p b m i", b=2, i=2),
+            )
+
+        def transpose_h(k):
+            gi, pos = group_of[k]
+            tp = ps_t.tile([P, 512], F32, name="tp", tag="tp")
+            for b in range(2):
+                for i in range(2):
+                    dst = (2 * b + i) * P
+                    nc.tensor.transpose(tp[:, dst:dst + P], h_of[gi][:, b, pos, i, :], ident[:])
+            nc.scalar.copy(
+                out=g2_of[k][:].rearrange("p (b m t) -> p b m t", b=2, t=4)[:, :, :, 0:2],
+                in_=tp[:].rearrange("p (b i m) -> p b m i", b=2, i=2),
+            )
+
+        def quantise_hs(k):
+            g2c = g2c_pool.tile([P, 256], U32, name="g2c", tag="g2c", align_bytes=64)
+            g2s = g2c_pool.tile([P, 256], U8, name="g2s", tag="g2s", align_bytes=64)
+            nc.vector.quantize_mx(out=g2c[:].bitcast(FP8X4), scales=g2s[:], in_=g2_of[k][:])
+            g2q_of[k] = (g2c, g2s)
 
         def gate_passes(k):
-            st = state_of[k]
-            ob = ps_o.tile([P, 512], F32, name="ob", tag="ob")
+            gi, pos = group_of[k]
+            g2c, g2s = g2q_of[k]
+            ob = ps_m.tile([P, 512], F32, name="mx", tag="mx")
             for b in range(2):
                 nc.tensor.matmul_mx(
                     out=ob[:, 256 * b:256 * b + 256],
-                    lhsT=st["g2c"][:, P * b:P * b + P].bitcast(FP8X4),
-                    lhsT_scale=st["g2s"][:, P * b:P * b + P],
+                    lhsT=g2c[:, P * b:P * b + P].bitcast(FP8X4),
+                    lhsT_scale=g2s[:, P * b:P * b + P],
                     rhs=wc[:].bitcast(FP8X4),
                     rhs_scale=ws[:],
                     start=True,
                     stop=True,
                 )
-            return ob
-
-        def gate_sigmoid(k, ob):
-            if k % 2 == 0:
-                ru = out_pool.tile([P, 2, 2, 2, P], F32, name="ru", tag="ru")
-                pair_tiles[("ru", k // 2)] = ru
-            ru = pair_tiles[("ru", k // 2)]
+            if pos == 0:
+                ru = ru_pool.tile([P, 2, 2, len(GROUPS[gi]), P], F32, name="ru", tag="ru")
+                ru_of[gi] = ru
             nc.scalar.activation(
-                out=ru[:, :, :, k % 2, :].rearrange("p r b u -> p b r u"),
+                out=ru_of[gi][:, :, :, pos, :].rearrange("p r b u -> p b r u"),
                 in_=ob[:].rearrange("p (b r u) -> p b r u", b=2, r=2),
                 func=SIGMOID,
             )
 
-        def store_h(q):
-            nc.sync.dma_start(
-                out=h_view[:, :, 2 * q:2 * q + 2, :],
-                in_=pair_tiles[("h", q)][:].rearrange("p b t i c -> p b t (i c)"),
-            )
+        def store_h(gi):
+            t0 = GROUPS[gi][0]
+            n = len(GROUPS[gi])
+            nc.sync.dma_start(out=h_view[:, :, t0:t0 + n, :], in_=h_of[gi][:].rearrange("p b t i c -> p b t (i c)"))
 
-        def store_ru(q):
-            ru = pair_tiles[("ru", q)]
-            nc.sync.dma_start(out=r_view[:, :, 2 * q:2 * q + 2, :], in_=ru[:, 0])
-            nc.sync.dma_start(out=u_view[:, :, 2 * q:2 * q + 2, :], in_=ru[:, 1])
+        def store_ru(gi):
+            t0 = GROUPS[gi][0]
+            n = len(GROUPS[gi])
+            nc.sync.dma_start(out=r_view[:, :, t0:t0 + n, :], in_=ru_of[gi][:, 0])
+            nc.sync.dma_start(out=u_view[:, :, t0:t0 + n, :], in_=ru_of[gi][:, 1])
 
         prepare_x(0)
-        plain_half(None, 0, 0)
-        plain_half(None, 0, 1)
+        xr[(1, 0)] = load_x(1, 0)
+        xr[(1, 1)] = load_x(1, 1)
+        load_sup(1)
+        wraw = const.tile([P, 2, 4, P], BF16, name="wraw", tag="wraw")
+        nc.sync.dma_start(out=wraw[:, 0], in_=r_kernel.rearrange("(t p) u -> p t u", p=P))
+        nc.sync.dma_start(out=wraw[:, 1], in_=u_kernel.rearrange("(t p) u -> p t u", p=P))
+        for k in range(2, RAW_BUFS):
+            load_sup(k)
+        transpose_sup(0, 0)
+        quantise_sup(0)
         prepare_x(1)
 
         wg = const.tile([P, 2, P, 4], BF16, name="wg", tag="wg", align_bytes=64)
         wc = const.tile([P, 256], U32, name="wc", tag="wc", align_bytes=64)
         ws = const.tile([P, 256], U8, name="ws", tag="ws", align_bytes=64)
 
-        for it in range(NBLK + 1):
-            k_h = it - 1 if it >= 1 else None
-            k_t = it + 1 if it + 1 < NBLK else None
-            plain_half(k_h, k_t, 0)
-            if it < NBLK:
-                feats_passes(it)
-            plain_half(k_h, k_t, 1)
-            if it == 0:
+        n_groups = len(GROUPS)
+        for j in range(n_groups + 1):
+            before = GROUPS[j - 1] if j >= 1 else ()
+            now = GROUPS[j] if j < n_groups else ()
+            after = GROUPS[j + 1] if j + 1 < n_groups else ()
+            for pos in range(max(len(before), len(after))):
+                if pos < len(after):
+                    transpose_sup(after[pos], pos)
+                if pos < len(before):
+                    transpose_h(before[pos])
+            for k in before:
+                quantise_hs(k)
+            for k in after:
+                quantise_sup(k)
+            if j == 0:
                 nc.vector.tensor_copy(out=wg[:], in_=wraw[:].rearrange("p r t u -> p r u t"))
                 nc.vector.quantize_mx(out=wc[:].bitcast(FP8X4), scales=ws[:], in_=wg[:].rearrange("p r u t -> p (r u t)"))
-            if it < NBLK:
-                prev_passes(it)
-            if it >= 1:
-                ob = gate_passes(it - 1)
-                gate_sigmoid(it - 1, ob)
-            if it < NBLK and it % 2 == 1:
-                store_h(it // 2)
-            if it >= 1 and (it - 1) % 2 == 1:
-                store_ru((it - 1) // 2)
+            for pos in range(max(len(before), len(now))):
+                if pos < len(now):
+                    feats_passes(now[pos])
+                    prev_passes(now[pos])
+                if pos < len(before):
+                    gate_passes(before[pos])
+            if j < n_groups:
+                store_h(j)
+            if j >= 1:
+                store_ru(j - 1)

@@ -14,7 +14,6 @@ P = 128
 NODES = 2048
 NBLK = 16
 RAW_BUFS = 8
-GROUPS = ((0,), (1,), (2, 3), (4, 5), (6, 7), (8, 9), (10, 11), (12, 13), (14,), (15,))
 FLOPS = 2 * 2 * 512 * NODES * NODES + 2 * 4096 * 512 * 256
 
 
@@ -22,16 +21,16 @@ def tile_gcrnncell_pa_kernel(tc, inputs, state, support0, support1, r_kernel, u_
     nc = tc.nc
     with ExitStack() as ctx:
         const = ctx.enter_context(tc.tile_pool(name="const", bufs=1))
-        xraw_pool = ctx.enter_context(tc.tile_pool(name="xraw", bufs=2))
+        xraw_pool = ctx.enter_context(tc.tile_pool(name="xraw", bufs=4))
         raw_pool = ctx.enter_context(tc.tile_pool(name="raw", bufs=RAW_BUFS))
-        grp_pool = ctx.enter_context(tc.tile_pool(name="grp", bufs=4))
-        code_pool = ctx.enter_context(tc.tile_pool(name="code", bufs=7))
-        g2_pool = ctx.enter_context(tc.tile_pool(name="g2p", bufs=6))
-        g2c_pool = ctx.enter_context(tc.tile_pool(name="g2cp", bufs=4))
-        h_pool = ctx.enter_context(tc.tile_pool(name="hp", bufs=3))
-        ru_pool = ctx.enter_context(tc.tile_pool(name="rup", bufs=2))
-        ps_t = ctx.enter_context(tc.psum_pool(name="pst", bufs=5))
-        ps_m = ctx.enter_context(tc.psum_pool(name="psm", bufs=3))
+        grp_pool = ctx.enter_context(tc.tile_pool(name="grp", bufs=2))
+        code_pool = ctx.enter_context(tc.tile_pool(name="code", bufs=3))
+        hs_pool = ctx.enter_context(tc.tile_pool(name="hs", bufs=2))
+        out_pool = ctx.enter_context(tc.tile_pool(name="outs", bufs=3))
+        ps_t = ctx.enter_context(tc.psum_pool(name="pst", bufs=4))
+        ps_g = ctx.enter_context(tc.psum_pool(name="psg", bufs=1))
+        ps_h = ctx.enter_context(tc.psum_pool(name="psh", bufs=2))
+        ps_o = ctx.enter_context(tc.psum_pool(name="pso", bufs=1))
         ctx.enter_context(tc.manual_schedule())
 
         sup_view = [s.rearrange("(p t) n -> p t n", t=NBLK) for s in (support0, support1)]
@@ -40,17 +39,20 @@ def tile_gcrnncell_pa_kernel(tc, inputs, state, support0, support1, r_kernel, u_
         u_view = out_1.rearrange("b (p t) u -> p b t u", t=NBLK)
         h_view = out_2.rearrange("b (p t) f -> p b t f", t=NBLK)
 
-        group_of = {}
-        for gi, blocks in enumerate(GROUPS):
-            for pos, k in enumerate(blocks):
-                group_of[k] = (gi, pos)
-
         ident = const.tile([P, P], F32, name="ident", tag="ident")
         make_identity(nc, ident[:])
         warm_in = const.tile([P, 1], F32, name="warm_in", tag="warm_in")
         warm_out = const.tile([P, 1], F32, name="warm_out", tag="warm_out")
         nc.vector.memset(warm_in[:], 0.0)
         nc.scalar.activation(out=warm_out[:], in_=warm_in[:], func=SIGMOID)
+
+        zeros = const.tile([P, 512], BF16, name="zeros", tag="zeros")
+        nc.vector.memset(zeros[:], 0.0)
+
+        def keep_clock(n):
+            tp = ps_t.tile([P, 512], F32, name="tp", tag="tp")
+            for d in range(n):
+                nc.tensor.matmul(out=tp[:], lhsT=zeros[:, 0:P], rhs=zeros[:], start=True, stop=True)
 
         raw = {}
 
@@ -75,12 +77,20 @@ def tile_gcrnncell_pa_kernel(tc, inputs, state, support0, support1, r_kernel, u_
         xr[(0, 0)] = load_x(0, 0)
         xr[(0, 1)] = load_x(0, 1)
         load_sup(0)
+        xr[(1, 0)] = load_x(1, 0)
+        xr[(1, 1)] = load_x(1, 1)
+        load_sup(1)
+        wraw = const.tile([P, 2, 4, P], BF16, name="wraw", tag="wraw")
+        nc.sync.dma_start(out=wraw[:, 0], in_=r_kernel.rearrange("(t p) u -> p t u", p=P))
+        nc.sync.dma_start(out=wraw[:, 1], in_=u_kernel.rearrange("(t p) u -> p t u", p=P))
+        for k in range(2, RAW_BUFS):
+            load_sup(k)
 
         xcodes = []
         xscales = []
 
         def prepare_x(kind):
-            xg = grp_pool.tile([P, 4096], BF16, name="grouped", tag="grouped", align_bytes=64)
+            xg = const.tile([P, 4096], BF16, name="xg%d" % kind, tag="xg%d" % kind, align_bytes=64)
             xc = const.tile([P, 1024], U32, name="xc%d" % kind, tag="xc%d" % kind, align_bytes=64)
             xs = const.tile([P, 1024], U8, name="xs%d" % kind, tag="xs%d" % kind, align_bytes=64)
             xg32 = xg[:].bitcast(F32).rearrange("p (g b c u) -> p g b c u", g=4, b=2, u=2)
@@ -104,34 +114,23 @@ def tile_gcrnncell_pa_kernel(tc, inputs, state, support0, support1, r_kernel, u_
             xscales.append(xs)
 
         sup_codes = {}
-        grouped_of = {}
-        g2_of = {}
-        g2q_of = {}
-        h_of = {}
-        ru_of = {}
+        state_of = {}
 
-        def transpose_sup(k, pos):
-            grouped = grp_pool.tile([P, 4096], BF16, name="grouped", tag="grouped", align_bytes=64)
-            grouped_of[k] = grouped
-            engines = (0, pos % 2, 0, 1)
-            for g in range(4):
-                tp = ps_t.tile([P, 512], F32, name="tp", tag="tp")
-                for i in range(2):
-                    words = raw[(k, i)][:].bitcast(F32)
-                    for u in range(2):
-                        col = 256 * g + 128 * u
-                        dst = (2 * i + u) * P
-                        nc.tensor.transpose(tp[:, dst:dst + P], words[:, col:col + P], ident[:])
-                copy_on(
-                    engines[g],
-                    grouped[:].bitcast(F32)[:, 512 * g:512 * g + 512].rearrange("p (i m u) -> p i m u", i=2, u=2),
-                    tp[:].rearrange("p (i u m) -> p i m u", i=2, u=2),
-                )
-            if k + RAW_BUFS < NBLK:
-                load_sup(k + RAW_BUFS)
+        def transpose_bank(k, g, grouped):
+            tp = ps_t.tile([P, 512], F32, name="tp", tag="tp")
+            for i in range(2):
+                words = raw[(k, i)][:].bitcast(F32)
+                for u in range(2):
+                    col = 256 * g + 128 * u
+                    dst = (2 * i + u) * P
+                    nc.tensor.transpose(tp[:, dst:dst + P], words[:, col:col + P], ident[:])
+            copy_on(
+                g % 2,
+                grouped[:].bitcast(F32)[:, 512 * g:512 * g + 512].rearrange("p (i m u) -> p i m u", i=2, u=2),
+                tp[:].rearrange("p (i u m) -> p i m u", i=2, u=2),
+            )
 
-        def quantise_sup(k):
-            grouped = grouped_of[k]
+        def quantise_sup(k, grouped):
             sc = code_pool.tile([P, 1024], U32, name="sc", tag="sc", align_bytes=64)
             ss = code_pool.tile([P, 1024], U8, name="ss", tag="ss", align_bytes=64)
             for half in range(2):
@@ -142,10 +141,46 @@ def tile_gcrnncell_pa_kernel(tc, inputs, state, support0, support1, r_kernel, u_
                 )
             sup_codes[k] = (sc, ss)
 
+        def quantise_hs(k):
+            g2 = state_of[k]["g2"]
+            g2c = hs_pool.tile([P, 256], U32, name="g2c", tag="g2c", align_bytes=64)
+            g2s = hs_pool.tile([P, 256], U8, name="g2s", tag="g2s", align_bytes=64)
+            nc.vector.quantize_mx(out=g2c[:].bitcast(FP8X4), scales=g2s[:], in_=g2[:])
+            state_of[k]["g2c"] = g2c
+            state_of[k]["g2s"] = g2s
+
+        def plain_phase(k_h, k_t):
+            if k_h is not None:
+                st = state_of[k_h]
+                g2 = hs_pool.tile([P, 1024], BF16, name="g2", tag="g2", align_bytes=64)
+                st["g2"] = g2
+                for b in range(2):
+                    for i in range(2):
+                        nc.tensor.transpose(st["H"][b][:, i * P:(i + 1) * P], st["h32"][:, b, k_h % 2, i, :], ident[:])
+                    copy_on(
+                        b,
+                        g2[:, 512 * b:512 * b + 512].rearrange("p (m t) -> p m t", t=4),
+                        st["H"][b][:].rearrange("p (t m) -> p m t", t=4),
+                    )
+            if k_t is not None:
+                grouped = grp_pool.tile([P, 4096], BF16, name="grouped", tag="grouped", align_bytes=64)
+                transpose_bank(k_t, 0, grouped)
+                transpose_bank(k_t, 1, grouped)
+                if k_h is not None:
+                    quantise_hs(k_h)
+                transpose_bank(k_t, 2, grouped)
+                transpose_bank(k_t, 3, grouped)
+                quantise_sup(k_t, grouped)
+                if k_t + RAW_BUFS < NBLK:
+                    load_sup(k_t + RAW_BUFS)
+            elif k_h is not None:
+                quantise_hs(k_h)
+
+        pair_tiles = {}
+
         def feats_passes(k):
-            gi, pos = group_of[k]
             sc, ss = sup_codes[k]
-            gb = ps_m.tile([P, 512], F32, name="mx", tag="mx")
+            gb = ps_g.tile([P, 512], F32, name="gb", tag="gb")
             for i in range(2):
                 for g in range(4):
                     a = (2 * g + i) * P
@@ -158,19 +193,22 @@ def tile_gcrnncell_pa_kernel(tc, inputs, state, support0, support1, r_kernel, u_
                         start=(g == 0),
                         stop=(g == 3),
                     )
-            if pos == 0:
-                h32 = h_pool.tile([P, 2, len(GROUPS[gi]), 2, P], F32, name="h32", tag="h32")
-                h_of[gi] = h32
-            nc.scalar.copy(out=h_of[gi][:, :, pos, :, :], in_=gb[:].rearrange("p (i b c) -> p b i c", i=2, b=2))
+            if k % 2 == 0:
+                h32 = out_pool.tile([P, 2, 2, 2, P], F32, name="h32", tag="h32")
+                pair_tiles[("h", k // 2)] = h32
+            h32 = pair_tiles[("h", k // 2)]
+            nc.scalar.copy(out=h32[:, :, k % 2, :, :], in_=gb[:].rearrange("p (i b c) -> p b i c", i=2, b=2))
+            state_of[k] = {"h32": h32}
 
         def prev_passes(k):
             sc, ss = sup_codes[k]
-            sb = ps_m.tile([P, 512], F32, name="mx", tag="mx")
+            banks = []
             for b in range(2):
+                hb = ps_h.tile([P, 512], F32, name="hb", tag="hb")
                 for g in range(4):
                     a = (2 * g + b) * P
                     nc.tensor.matmul_mx(
-                        out=sb[:, 256 * b:256 * b + 256],
+                        out=hb[:, 256:512],
                         lhsT=xcodes[1][:, a:a + P].bitcast(FP8X4),
                         lhsT_scale=xscales[1][:, a:a + P],
                         rhs=sc[:, 256 * g:256 * g + 256].bitcast(FP8X4),
@@ -178,38 +216,77 @@ def tile_gcrnncell_pa_kernel(tc, inputs, state, support0, support1, r_kernel, u_
                         start=(g == 0),
                         stop=(g == 3),
                     )
-            g2 = g2_pool.tile([P, 1024], BF16, name="g2", tag="g2", align_bytes=64)
-            g2_of[k] = g2
-            nc.scalar.copy(
-                out=g2[:].rearrange("p (b m t) -> p b m t", b=2, t=4)[:, :, :, 2:4],
-                in_=sb[:].rearrange("p (b i m) -> p b m i", b=2, i=2),
-            )
-
-        def transpose_h(k):
-            gi, pos = group_of[k]
-            tp = ps_t.tile([P, 512], F32, name="tp", tag="tp")
-            for b in range(2):
-                for i in range(2):
-                    dst = (2 * b + i) * P
-                    nc.tensor.transpose(tp[:, dst:dst + P], h_of[gi][:, b, pos, i, :], ident[:])
-            nc.scalar.copy(
-                out=g2_of[k][:].rearrange("p (b m t) -> p b m t", b=2, t=4)[:, :, :, 0:2],
-                in_=tp[:].rearrange("p (b i m) -> p b m i", b=2, i=2),
-            )
-
-        def quantise_hs(k):
-            g2c = g2c_pool.tile([P, 256], U32, name="g2c", tag="g2c", align_bytes=64)
-            g2s = g2c_pool.tile([P, 256], U8, name="g2s", tag="g2s", align_bytes=64)
-            nc.vector.quantize_mx(out=g2c[:].bitcast(FP8X4), scales=g2s[:], in_=g2_of[k][:])
-            g2q_of[k] = (g2c, g2s)
+                banks.append(hb)
+            state_of[k]["H"] = banks
 
         def gate_passes(k):
-            gi, pos = group_of[k]
-            g2c, g2s = g2q_of[k]
-            ob = ps_m.tile([P, 512], F32, name="mx", tag="mx")
+            st = state_of[k]
+            ob = ps_o.tile([P, 512], F32, name="ob", tag="ob")
             for b in range(2):
                 nc.tensor.matmul_mx(
                     out=ob[:, 256 * b:256 * b + 256],
+                    lhsT=st["g2c"][:, P * b:P * b + P].bitcast(FP8X4),
+                    lhsT_scale=st["g2s"][:, P * b:P * b + P],
+                    rhs=wc[:].bitcast(FP8X4),
+                    rhs_scale=ws[:],
+                    start=True,
+                    stop=True,
+                )
+            return ob
+
+        def gate_sigmoid(k, ob):
+            if k % 2 == 0:
+                ru = out_pool.tile([P, 2, 2, 2, P], F32, name="ru", tag="ru")
+                pair_tiles[("ru", k // 2)] = ru
+            ru = pair_tiles[("ru", k // 2)]
+            nc.scalar.activation(
+                out=ru[:, :, :, k % 2, :].rearrange("p r b u -> p b r u"),
+                in_=ob[:].rearrange("p (b r u) -> p b r u", b=2, r=2),
+                func=SIGMOID,
+            )
+
+        def store_h(q):
+            nc.sync.dma_start(
+                out=h_view[:, :, 2 * q:2 * q + 2, :],
+                in_=pair_tiles[("h", q)][:].rearrange("p b t i c -> p b t (i c)"),
+            )
+
+        def store_ru(q):
+            ru = pair_tiles[("ru", q)]
+            nc.sync.dma_start(out=r_view[:, :, 2 * q:2 * q + 2, :], in_=ru[:, 0])
+            nc.sync.dma_start(out=u_view[:, :, 2 * q:2 * q + 2, :], in_=ru[:, 1])
+
+        def store_ru_block(k):
+            ru = pair_tiles[("ru", k // 2)]
+            nc.sync.dma_start(out=r_view[:, :, k, :], in_=ru[:, 0, :, k % 2, :])
+            nc.sync.dma_start(out=u_view[:, :, k, :], in_=ru[:, 1, :, k % 2, :])
+
+        def last_block(k):
+            st = state_of[k]
+            ru = pair_tiles[("ru", k // 2)]
+            g2 = hs_pool.tile([P, 1024], BF16, name="g2", tag="g2", align_bytes=64)
+            g2c = hs_pool.tile([P, 256], U32, name="g2c", tag="g2c", align_bytes=64)
+            g2s = hs_pool.tile([P, 256], U8, name="g2s", tag="g2s", align_bytes=64)
+            ob0 = ps_o.tile([P, 512], F32, name="ob", tag="ob")
+            ob1 = ps_g.tile([P, 512], F32, name="gb", tag="gb")
+            banks = (ob0, ob1)
+            for b in range(2):
+                for i in range(2):
+                    nc.tensor.transpose(st["H"][b][:, i * P:(i + 1) * P], st["h32"][:, b, k % 2, i, :], ident[:])
+                copy_on(
+                    b,
+                    g2[:, 512 * b:512 * b + 512].rearrange("p (m t) -> p m t", t=4),
+                    st["H"][b][:].rearrange("p (t m) -> p m t", t=4),
+                )
+            for b in range(2):
+                nc.vector.quantize_mx(
+                    out=g2c[:, P * b:P * b + P].bitcast(FP8X4),
+                    scales=g2s[:, P * b:P * b + P],
+                    in_=g2[:, 512 * b:512 * b + 512],
+                )
+            for b in range(2):
+                nc.tensor.matmul_mx(
+                    out=banks[b][:, 0:256],
                     lhsT=g2c[:, P * b:P * b + P].bitcast(FP8X4),
                     lhsT_scale=g2s[:, P * b:P * b + P],
                     rhs=wc[:].bitcast(FP8X4),
@@ -217,67 +294,43 @@ def tile_gcrnncell_pa_kernel(tc, inputs, state, support0, support1, r_kernel, u_
                     start=True,
                     stop=True,
                 )
-            if pos == 0:
-                ru = ru_pool.tile([P, 2, 2, len(GROUPS[gi]), P], F32, name="ru", tag="ru")
-                ru_of[gi] = ru
-            nc.scalar.activation(
-                out=ru_of[gi][:, :, :, pos, :].rearrange("p r b u -> p b r u"),
-                in_=ob[:].rearrange("p (b r u) -> p b r u", b=2, r=2),
-                func=SIGMOID,
-            )
+                nc.scalar.activation(
+                    out=ru[:, :, b, k % 2, :],
+                    in_=banks[b][:, 0:256].rearrange("p (r u) -> p r u", r=2),
+                    func=SIGMOID,
+                )
+                nc.sync.dma_start(out=r_view[:, b, k, :], in_=ru[:, 0, b, k % 2, :])
+                if b == 0:
+                    nc.sync.dma_start(out=u_view[:, b, k, :], in_=ru[:, 1, b, k % 2, :])
+                else:
+                    nc.scalar.dma_start(out=u_view[:, b, k, :], in_=ru[:, 1, b, k % 2, :])
 
-        def store_h(gi):
-            t0 = GROUPS[gi][0]
-            n = len(GROUPS[gi])
-            nc.sync.dma_start(out=h_view[:, :, t0:t0 + n, :], in_=h_of[gi][:].rearrange("p b t i c -> p b t (i c)"))
-
-        def store_ru(gi):
-            t0 = GROUPS[gi][0]
-            n = len(GROUPS[gi])
-            nc.sync.dma_start(out=r_view[:, :, t0:t0 + n, :], in_=ru_of[gi][:, 0])
-            nc.sync.dma_start(out=u_view[:, :, t0:t0 + n, :], in_=ru_of[gi][:, 1])
-
+        keep_clock(6)
         prepare_x(0)
-        xr[(1, 0)] = load_x(1, 0)
-        xr[(1, 1)] = load_x(1, 1)
-        load_sup(1)
-        wraw = const.tile([P, 2, 4, P], BF16, name="wraw", tag="wraw")
-        nc.sync.dma_start(out=wraw[:, 0], in_=r_kernel.rearrange("(t p) u -> p t u", p=P))
-        nc.sync.dma_start(out=wraw[:, 1], in_=u_kernel.rearrange("(t p) u -> p t u", p=P))
-        for k in range(2, RAW_BUFS):
-            load_sup(k)
-        transpose_sup(0, 0)
-        quantise_sup(0)
+        keep_clock(3)
+        plain_phase(None, 0)
+        keep_clock(1)
         prepare_x(1)
+        keep_clock(3)
 
         wg = const.tile([P, 2, P, 4], BF16, name="wg", tag="wg", align_bytes=64)
         wc = const.tile([P, 256], U32, name="wc", tag="wc", align_bytes=64)
         ws = const.tile([P, 256], U8, name="ws", tag="ws", align_bytes=64)
 
-        n_groups = len(GROUPS)
-        for j in range(n_groups + 1):
-            before = GROUPS[j - 1] if j >= 1 else ()
-            now = GROUPS[j] if j < n_groups else ()
-            after = GROUPS[j + 1] if j + 1 < n_groups else ()
-            for pos in range(max(len(before), len(after))):
-                if pos < len(after):
-                    transpose_sup(after[pos], pos)
-                if pos < len(before):
-                    transpose_h(before[pos])
-            for k in before:
-                quantise_hs(k)
-            for k in after:
-                quantise_sup(k)
-            if j == 0:
+        for it in range(NBLK):
+            plain_phase(it - 1 if it >= 1 else None, it + 1 if it + 1 < NBLK else None)
+            if it == 0:
                 nc.vector.tensor_copy(out=wg[:], in_=wraw[:].rearrange("p r t u -> p r u t"))
                 nc.vector.quantize_mx(out=wc[:].bitcast(FP8X4), scales=ws[:], in_=wg[:].rearrange("p r u t -> p (r u t)"))
-            for pos in range(max(len(before), len(now))):
-                if pos < len(now):
-                    feats_passes(now[pos])
-                    prev_passes(now[pos])
-                if pos < len(before):
-                    gate_passes(before[pos])
-            if j < n_groups:
-                store_h(j)
-            if j >= 1:
-                store_ru(j - 1)
+            feats_passes(it)
+            if it >= 1:
+                ob = gate_passes(it - 1)
+                gate_sigmoid(it - 1, ob)
+            prev_passes(it)
+            if it % 2 == 1:
+                store_h(it // 2)
+            if it >= 1 and (it - 1) % 2 == 1:
+                store_ru((it - 1) // 2)
+            if it == NBLK - 1:
+                store_ru_block(it - 1)
+        last_block(NBLK - 1)

@@ -23,13 +23,12 @@ def tile_gcrnncell_pa_kernel(tc, inputs, state, support0, support1, r_kernel, u_
         const = ctx.enter_context(tc.tile_pool(name="const", bufs=1))
         xraw_pool = ctx.enter_context(tc.tile_pool(name="xraw", bufs=4))
         raw_pool = ctx.enter_context(tc.tile_pool(name="raw", bufs=RAW_BUFS))
-        grp_pool = ctx.enter_context(tc.tile_pool(name="grp", bufs=2))
-        code_pool = ctx.enter_context(tc.tile_pool(name="code", bufs=3))
-        hs_pool = ctx.enter_context(tc.tile_pool(name="hs", bufs=2))
+        grp_pool = ctx.enter_context(tc.tile_pool(name="grp", bufs=3))
+        code_pool = ctx.enter_context(tc.tile_pool(name="code", bufs=4))
+        hs_pool = ctx.enter_context(tc.tile_pool(name="hs", bufs=4))
         out_pool = ctx.enter_context(tc.tile_pool(name="outs", bufs=3))
-        ps_t = ctx.enter_context(tc.psum_pool(name="pst", bufs=4))
+        ring = ctx.enter_context(tc.psum_pool(name="ring", bufs=6))
         ps_g = ctx.enter_context(tc.psum_pool(name="psg", bufs=1))
-        ps_h = ctx.enter_context(tc.psum_pool(name="psh", bufs=2))
         ps_o = ctx.enter_context(tc.psum_pool(name="pso", bufs=1))
         ctx.enter_context(tc.manual_schedule())
 
@@ -50,7 +49,7 @@ def tile_gcrnncell_pa_kernel(tc, inputs, state, support0, support1, r_kernel, u_
         nc.vector.memset(zeros[:], 0.0)
 
         def keep_clock(n):
-            tp = ps_t.tile([P, 512], F32, name="tp", tag="tp")
+            tp = ring.tile([P, 512], F32, name="tp", tag="bank")
             for d in range(n):
                 nc.tensor.matmul(out=tp[:], lhsT=zeros[:, 0:P], rhs=zeros[:], start=True, stop=True)
 
@@ -97,7 +96,7 @@ def tile_gcrnncell_pa_kernel(tc, inputs, state, support0, support1, r_kernel, u_
             for b in range(2):
                 words = xr[(kind, b)][:].bitcast(F32)
                 for gp in range(2):
-                    tp = ps_t.tile([P, 512], F32, name="tp", tag="tp")
+                    tp = ring.tile([P, 512], F32, name="tp", tag="bank")
                     for gg in range(2):
                         for u in range(2):
                             col = 256 * (2 * gp + gg) + 128 * u
@@ -117,7 +116,7 @@ def tile_gcrnncell_pa_kernel(tc, inputs, state, support0, support1, r_kernel, u_
         state_of = {}
 
         def transpose_bank(k, g, grouped):
-            tp = ps_t.tile([P, 512], F32, name="tp", tag="tp")
+            tp = ring.tile([P, 512], F32, name="tp", tag="bank")
             for i in range(2):
                 words = raw[(k, i)][:].bitcast(F32)
                 for u in range(2):
@@ -149,32 +148,35 @@ def tile_gcrnncell_pa_kernel(tc, inputs, state, support0, support1, r_kernel, u_
             state_of[k]["g2c"] = g2c
             state_of[k]["g2s"] = g2s
 
-        def plain_phase(k_h, k_t):
-            if k_h is not None:
-                st = state_of[k_h]
+        def plain_phase(h_blocks, t_blocks):
+            for k in h_blocks:
+                st = state_of[k]
                 g2 = hs_pool.tile([P, 1024], BF16, name="g2", tag="g2", align_bytes=64)
                 st["g2"] = g2
                 for b in range(2):
                     for i in range(2):
-                        nc.tensor.transpose(st["H"][b][:, i * P:(i + 1) * P], st["h32"][:, b, k_h % 2, i, :], ident[:])
+                        nc.tensor.transpose(st["H"][b][:, i * P:(i + 1) * P], st["h32"][:, b, k % 2, i, :], ident[:])
                     copy_on(
                         b,
                         g2[:, 512 * b:512 * b + 512].rearrange("p (m t) -> p m t", t=4),
                         st["H"][b][:].rearrange("p (t m) -> p m t", t=4),
                     )
-            if k_t is not None:
-                grouped = grp_pool.tile([P, 4096], BF16, name="grouped", tag="grouped", align_bytes=64)
-                transpose_bank(k_t, 0, grouped)
-                transpose_bank(k_t, 1, grouped)
-                if k_h is not None:
-                    quantise_hs(k_h)
-                transpose_bank(k_t, 2, grouped)
-                transpose_bank(k_t, 3, grouped)
-                quantise_sup(k_t, grouped)
-                if k_t + RAW_BUFS < NBLK:
-                    load_sup(k_t + RAW_BUFS)
-            elif k_h is not None:
-                quantise_hs(k_h)
+            grouped = []
+            for n, k in enumerate(t_blocks):
+                gt = grp_pool.tile([P, 4096], BF16, name="grouped", tag="grouped", align_bytes=64)
+                grouped.append(gt)
+                for g in range(4):
+                    transpose_bank(k, g, gt)
+                if k + RAW_BUFS < NBLK:
+                    load_sup(k + RAW_BUFS)
+                if n == 0:
+                    for j in h_blocks:
+                        quantise_hs(j)
+            if not t_blocks:
+                for j in h_blocks:
+                    quantise_hs(j)
+            for k, gt in zip(t_blocks, grouped):
+                quantise_sup(k, gt)
 
         pair_tiles = {}
 
@@ -204,7 +206,7 @@ def tile_gcrnncell_pa_kernel(tc, inputs, state, support0, support1, r_kernel, u_
             sc, ss = sup_codes[k]
             banks = []
             for b in range(2):
-                hb = ps_h.tile([P, 512], F32, name="hb", tag="hb")
+                hb = ring.tile([P, 512], F32, name="hb", tag="bank")
                 for g in range(4):
                     a = (2 * g + b) * P
                     nc.tensor.matmul_mx(
@@ -308,7 +310,7 @@ def tile_gcrnncell_pa_kernel(tc, inputs, state, support0, support1, r_kernel, u_
         keep_clock(6)
         prepare_x(0)
         keep_clock(3)
-        plain_phase(None, 0)
+        plain_phase([], [0])
         keep_clock(1)
         prepare_x(1)
         keep_clock(3)
@@ -317,20 +319,36 @@ def tile_gcrnncell_pa_kernel(tc, inputs, state, support0, support1, r_kernel, u_
         wc = const.tile([P, 256], U32, name="wc", tag="wc", align_bytes=64)
         ws = const.tile([P, 256], U8, name="ws", tag="ws", align_bytes=64)
 
-        for it in range(NBLK):
-            plain_phase(it - 1 if it >= 1 else None, it + 1 if it + 1 < NBLK else None)
-            if it == 0:
-                nc.vector.tensor_copy(out=wg[:], in_=wraw[:].rearrange("p r t u -> p r u t"))
-                nc.vector.quantize_mx(out=wc[:].bitcast(FP8X4), scales=ws[:], in_=wg[:].rearrange("p r u t -> p (r u t)"))
-            feats_passes(it)
-            if it >= 1:
-                ob = gate_passes(it - 1)
-                gate_sigmoid(it - 1, ob)
-            prev_passes(it)
-            if it % 2 == 1:
-                store_h(it // 2)
-            if it >= 1 and (it - 1) % 2 == 1:
-                store_ru((it - 1) // 2)
-            if it == NBLK - 1:
-                store_ru_block(it - 1)
+        def mx_block(k, gate_k):
+            feats_passes(k)
+            if gate_k is not None:
+                ob = gate_passes(gate_k)
+                gate_sigmoid(gate_k, ob)
+            prev_passes(k)
+            if k % 2 == 1:
+                store_h(k // 2)
+            if gate_k is not None and gate_k % 2 == 1:
+                store_ru(gate_k // 2)
+
+        plain_phase([], [1])
+        nc.vector.tensor_copy(out=wg[:], in_=wraw[:].rearrange("p r t u -> p r u t"))
+        nc.vector.quantize_mx(out=wc[:].bitcast(FP8X4), scales=ws[:], in_=wg[:].rearrange("p r u t -> p (r u t)"))
+        mx_block(0, None)
+        plain_phase([0], [2])
+        mx_block(1, 0)
+        plain_phase([1], [3, 4])
+        mx_block(2, 1)
+        mx_block(3, None)
+        for a in range(2, NBLK - 4, 2):
+            plain_phase([a, a + 1], [a + 3, a + 4])
+            mx_block(a + 2, a)
+            mx_block(a + 3, a + 1)
+        plain_phase([NBLK - 4, NBLK - 3], [NBLK - 1])
+        mx_block(NBLK - 2, NBLK - 4)
+        ob = gate_passes(NBLK - 3)
+        gate_sigmoid(NBLK - 3, ob)
+        store_ru((NBLK - 3) // 2)
+        plain_phase([NBLK - 2], [])
+        mx_block(NBLK - 1, NBLK - 2)
+        store_ru_block(NBLK - 2)
         last_block(NBLK - 1)

@@ -13,7 +13,7 @@ SIGMOID = mybir.ActivationFunctionType.Sigmoid
 P = 128
 NODES = 2048
 NBLK = 16
-RAW_BUFS = 8
+RAW_BUFS = 9
 FLOPS = 2 * 2 * 512 * NODES * NODES + 2 * 4096 * 512 * 256
 
 
@@ -21,10 +21,10 @@ def tile_gcrnncell_pa_kernel(tc, inputs, state, support0, support1, r_kernel, u_
     nc = tc.nc
     with ExitStack() as ctx:
         const = ctx.enter_context(tc.tile_pool(name="const", bufs=1))
-        xraw_pool = ctx.enter_context(tc.tile_pool(name="xraw", bufs=4))
         raw_pool = ctx.enter_context(tc.tile_pool(name="raw", bufs=RAW_BUFS))
-        grp_pool = ctx.enter_context(tc.tile_pool(name="grp", bufs=3))
-        code_pool = ctx.enter_context(tc.tile_pool(name="code", bufs=4))
+        half_pool = ctx.enter_context(tc.tile_pool(name="half", bufs=4))
+        grp_pool = ctx.enter_context(tc.tile_pool(name="grp", bufs=4))
+        code_pool = ctx.enter_context(tc.tile_pool(name="code", bufs=6))
         hs_pool = ctx.enter_context(tc.tile_pool(name="hs", bufs=4))
         out_pool = ctx.enter_context(tc.tile_pool(name="outs", bufs=3))
         ring = ctx.enter_context(tc.psum_pool(name="ring", bufs=6))
@@ -48,17 +48,47 @@ def tile_gcrnncell_pa_kernel(tc, inputs, state, support0, support1, r_kernel, u_
         zeros = const.tile([P, 512], BF16, name="zeros", tag="zeros")
         nc.vector.memset(zeros[:], 0.0)
 
+        xc = const.tile([P, 2, 1024], U32, name="xc", tag="xc", align_bytes=64)
+        xs = const.tile([P, 2, 1024], U8, name="xs", tag="xs", align_bytes=64)
+        wraw = const.tile([P, 2, 4, P], BF16, name="wraw", tag="wraw")
+        wg = const.tile([P, 2, P, 4], BF16, name="wg", tag="wg", align_bytes=64)
+        wc = const.tile([P, 256], U32, name="wc", tag="wc", align_bytes=64)
+        ws = const.tile([P, 256], U8, name="ws", tag="ws", align_bytes=64)
+
         def keep_clock(n):
             tp = ring.tile([P, 512], F32, name="tp", tag="bank")
             for d in range(n):
                 nc.tensor.matmul(out=tp[:], lhsT=zeros[:, 0:P], rhs=zeros[:], start=True, stop=True)
 
         raw = {}
+        xr = {}
+        first_words = {}
 
-        def load_x(kind, b):
-            t = xraw_pool.tile([P, NODES], BF16, name="xraw", tag="xraw")
-            nc.sync.dma_start(out=t[:], in_=x_view[kind][b])
-            return t
+        def load_x(kind):
+            for b in range(2):
+                t = raw_pool.tile([P, NODES], BF16, name="raw%d" % b, tag="raw%d" % b)
+                nc.sync.dma_start(out=t[:], in_=x_view[kind][b])
+                for half in range(2):
+                    xr[(kind, b, half)] = t[:].bitcast(F32)[:, 512 * half:512 * half + 512]
+
+        def load_x_half(b, half):
+            t = half_pool.tile([P, 1024], BF16, name="xhalf", tag="xhalf")
+            nc.sync.dma_start(out=t[:], in_=x_view[0][b][:, 1024 * half:1024 * half + 1024])
+            xr[(0, b, half)] = t[:].bitcast(F32)
+
+        def load_first_sup_half(i, half):
+            t = half_pool.tile([P, 1024], BF16, name="shalf", tag="shalf")
+            nc.sync.dma_start(out=t[:], in_=sup_view[i][:, 0, 1024 * half:1024 * half + 1024])
+            first_words[(i, half)] = t[:].bitcast(F32)
+
+        def sup_words(k, i, g):
+            if k == 0:
+                return first_words[(i, g // 2)][:, 256 * (g % 2):256 * (g % 2) + 256]
+            return raw[(k, i)][:].bitcast(F32)[:, 256 * g:256 * g + 256]
+
+        def load_w():
+            for r, kern in enumerate((r_kernel, u_kernel)):
+                nc.sync.dma_start(out=wraw[:, r], in_=kern.rearrange("(t p) u -> p t u", p=P))
 
         def load_sup(k):
             for i in range(2):
@@ -72,73 +102,87 @@ def tile_gcrnncell_pa_kernel(tc, inputs, state, support0, support1, r_kernel, u_
             else:
                 nc.scalar.copy(out=out, in_=in_)
 
-        xr = {}
-        xr[(0, 0)] = load_x(0, 0)
-        xr[(0, 1)] = load_x(0, 1)
-        load_sup(0)
-        xr[(1, 0)] = load_x(1, 0)
-        xr[(1, 1)] = load_x(1, 1)
-        load_sup(1)
-        wraw = const.tile([P, 2, 4, P], BF16, name="wraw", tag="wraw")
-        nc.sync.dma_start(out=wraw[:, 0], in_=r_kernel.rearrange("(t p) u -> p t u", p=P))
-        nc.sync.dma_start(out=wraw[:, 1], in_=u_kernel.rearrange("(t p) u -> p t u", p=P))
-        for k in range(2, RAW_BUFS):
-            load_sup(k)
-
-        xcodes = []
-        xscales = []
-
         def prepare_x(kind):
-            xg = const.tile([P, 4096], BF16, name="xg%d" % kind, tag="xg%d" % kind, align_bytes=64)
-            xc = const.tile([P, 1024], U32, name="xc%d" % kind, tag="xc%d" % kind, align_bytes=64)
-            xs = const.tile([P, 1024], U8, name="xs%d" % kind, tag="xs%d" % kind, align_bytes=64)
+            xg = grp_pool.tile([P, 4096], BF16, name="grouped", tag="grouped", align_bytes=64)
             xg32 = xg[:].bitcast(F32).rearrange("p (g b c u) -> p g b c u", g=4, b=2, u=2)
-            for b in range(2):
-                words = xr[(kind, b)][:].bitcast(F32)
-                for gp in range(2):
+            for gp in range(2):
+                for b in range(2):
+                    words = xr[(kind, b, gp)]
                     tp = ring.tile([P, 512], F32, name="tp", tag="bank")
                     for gg in range(2):
                         for u in range(2):
-                            col = 256 * (2 * gp + gg) + 128 * u
+                            col = 256 * gg + 128 * u
                             dst = (2 * gg + u) * P
                             nc.tensor.transpose(tp[:, dst:dst + P], words[:, col:col + P], ident[:])
-                    copy_on(gp, xg32[:, 2 * gp:2 * gp + 2, b, :, :], tp[:].rearrange("p (g u c) -> p g c u", g=2, u=2))
+                    copy_on(b, xg32[:, 2 * gp:2 * gp + 2, b, :, :], tp[:].rearrange("p (g u c) -> p g c u", g=2, u=2))
             for half in range(2):
                 nc.vector.quantize_mx(
-                    out=xc[:, 512 * half:512 * half + 512].bitcast(FP8X4),
-                    scales=xs[:, 512 * half:512 * half + 512],
+                    out=xc[:, kind, 512 * half:512 * half + 512].bitcast(FP8X4),
+                    scales=xs[:, kind, 512 * half:512 * half + 512],
                     in_=xg[:, 2048 * half:2048 * half + 2048],
                 )
-            xcodes.append(xc)
-            xscales.append(xs)
 
         sup_codes = {}
+        grouped_of = {}
         state_of = {}
 
-        def transpose_bank(k, g, grouped):
+        def transpose_bank(k, g, grouped, which):
             tp = ring.tile([P, 512], F32, name="tp", tag="bank")
             for i in range(2):
-                words = raw[(k, i)][:].bitcast(F32)
+                words = sup_words(k, i, g)
                 for u in range(2):
-                    col = 256 * g + 128 * u
                     dst = (2 * i + u) * P
-                    nc.tensor.transpose(tp[:, dst:dst + P], words[:, col:col + P], ident[:])
+                    nc.tensor.transpose(tp[:, dst:dst + P], words[:, 128 * u:128 * u + 128], ident[:])
             copy_on(
-                g % 2,
+                which,
                 grouped[:].bitcast(F32)[:, 512 * g:512 * g + 512].rearrange("p (i m u) -> p i m u", i=2, u=2),
                 tp[:].rearrange("p (i u m) -> p i m u", i=2, u=2),
             )
 
-        def quantise_sup(k, grouped):
-            sc = code_pool.tile([P, 1024], U32, name="sc", tag="sc", align_bytes=64)
-            ss = code_pool.tile([P, 1024], U8, name="ss", tag="ss", align_bytes=64)
-            for half in range(2):
-                nc.vector.quantize_mx(
-                    out=sc[:, 512 * half:512 * half + 512].bitcast(FP8X4),
-                    scales=ss[:, 512 * half:512 * half + 512],
-                    in_=grouped[:, 2048 * half:2048 * half + 2048],
+        def new_grouped(k):
+            gt = grp_pool.tile([P, 4096], BF16, name="grouped", tag="grouped", align_bytes=64)
+            grouped_of[k] = gt
+
+        def turn_sup(k, engines=(0, 1, 0, 1)):
+            new_grouped(k)
+            for g in range(4):
+                transpose_bank(k, g, grouped_of[k], engines[g])
+
+        def quantise_half(k, half):
+            if half == 0:
+                sc = code_pool.tile([P, 1024], U32, name="sc", tag="sc", align_bytes=64)
+                ss = code_pool.tile([P, 1024], U8, name="ss", tag="ss", align_bytes=64)
+                sup_codes[k] = (sc, ss)
+            sc, ss = sup_codes[k]
+            nc.vector.quantize_mx(
+                out=sc[:, 512 * half:512 * half + 512].bitcast(FP8X4),
+                scales=ss[:, 512 * half:512 * half + 512],
+                in_=grouped_of[k][:, 2048 * half:2048 * half + 2048],
+            )
+
+        def quantise_sup(k):
+            quantise_half(k, 0)
+            quantise_half(k, 1)
+
+        def turn_h(k):
+            st = state_of[k]
+            st["H"] = []
+            for b in range(2):
+                hb = ring.tile([P, 512], F32, name="hb", tag="bank")
+                for i in range(2):
+                    nc.tensor.transpose(hb[:, i * P:(i + 1) * P], st["h32"][:, b, k % 2, i, :], ident[:])
+                st["H"].append(hb)
+
+        def regroup(k):
+            st = state_of[k]
+            g2 = hs_pool.tile([P, 1024], BF16, name="g2", tag="g2", align_bytes=64)
+            st["g2"] = g2
+            for b in range(2):
+                copy_on(
+                    b,
+                    g2[:, 512 * b:512 * b + 512].rearrange("p (m t) -> p m t", t=4),
+                    st["H"][b][:].rearrange("p (t m) -> p m t", t=4),
                 )
-            sup_codes[k] = (sc, ss)
 
         def quantise_hs(k):
             g2 = state_of[k]["g2"]
@@ -148,41 +192,11 @@ def tile_gcrnncell_pa_kernel(tc, inputs, state, support0, support1, r_kernel, u_
             state_of[k]["g2c"] = g2c
             state_of[k]["g2s"] = g2s
 
-        def plain_phase(h_blocks, t_blocks):
-            for k in h_blocks:
-                st = state_of[k]
-                g2 = hs_pool.tile([P, 1024], BF16, name="g2", tag="g2", align_bytes=64)
-                st["g2"] = g2
-                for b in range(2):
-                    for i in range(2):
-                        nc.tensor.transpose(st["H"][b][:, i * P:(i + 1) * P], st["h32"][:, b, k % 2, i, :], ident[:])
-                    copy_on(
-                        b,
-                        g2[:, 512 * b:512 * b + 512].rearrange("p (m t) -> p m t", t=4),
-                        st["H"][b][:].rearrange("p (t m) -> p m t", t=4),
-                    )
-            grouped = []
-            for n, k in enumerate(t_blocks):
-                gt = grp_pool.tile([P, 4096], BF16, name="grouped", tag="grouped", align_bytes=64)
-                grouped.append(gt)
-                for g in range(4):
-                    transpose_bank(k, g, gt)
-                if k + RAW_BUFS < NBLK:
-                    load_sup(k + RAW_BUFS)
-                if n == 0:
-                    for j in h_blocks:
-                        quantise_hs(j)
-            if not t_blocks:
-                for j in h_blocks:
-                    quantise_hs(j)
-            for k, gt in zip(t_blocks, grouped):
-                quantise_sup(k, gt)
-
         pair_tiles = {}
 
-        def feats_passes(k):
+        def feats_passes(k, pool=ps_g, tag="gb"):
             sc, ss = sup_codes[k]
-            gb = ps_g.tile([P, 512], F32, name="gb", tag="gb")
+            gb = pool.tile([P, 512], F32, name="gb", tag=tag)
             for i in range(2):
                 for g in range(4):
                     a = (2 * g + i) * P
@@ -190,8 +204,8 @@ def tile_gcrnncell_pa_kernel(tc, inputs, state, support0, support1, r_kernel, u_
                         out=gb[:, 256 * i:256 * i + 256],
                         lhsT=sc[:, a:a + P].bitcast(FP8X4),
                         lhsT_scale=ss[:, a:a + P],
-                        rhs=xcodes[0][:, 256 * g:256 * g + 256].bitcast(FP8X4),
-                        rhs_scale=xscales[0][:, 256 * g:256 * g + 256],
+                        rhs=xc[:, 0, 256 * g:256 * g + 256].bitcast(FP8X4),
+                        rhs_scale=xs[:, 0, 256 * g:256 * g + 256],
                         start=(g == 0),
                         stop=(g == 3),
                     )
@@ -204,22 +218,19 @@ def tile_gcrnncell_pa_kernel(tc, inputs, state, support0, support1, r_kernel, u_
 
         def prev_passes(k):
             sc, ss = sup_codes[k]
-            banks = []
             for b in range(2):
-                hb = ring.tile([P, 512], F32, name="hb", tag="bank")
+                hb = state_of[k]["H"][b]
                 for g in range(4):
                     a = (2 * g + b) * P
                     nc.tensor.matmul_mx(
                         out=hb[:, 256:512],
-                        lhsT=xcodes[1][:, a:a + P].bitcast(FP8X4),
-                        lhsT_scale=xscales[1][:, a:a + P],
+                        lhsT=xc[:, 1, a:a + P].bitcast(FP8X4),
+                        lhsT_scale=xs[:, 1, a:a + P],
                         rhs=sc[:, 256 * g:256 * g + 256].bitcast(FP8X4),
                         rhs_scale=ss[:, 256 * g:256 * g + 256],
                         start=(g == 0),
                         stop=(g == 3),
                     )
-                banks.append(hb)
-            state_of[k]["H"] = banks
 
         def gate_passes(k):
             st = state_of[k]
@@ -247,6 +258,10 @@ def tile_gcrnncell_pa_kernel(tc, inputs, state, support0, support1, r_kernel, u_
                 func=SIGMOID,
             )
 
+        def gates(k):
+            ob = gate_passes(k)
+            gate_sigmoid(k, ob)
+
         def store_h(q):
             nc.sync.dma_start(
                 out=h_view[:, :, 2 * q:2 * q + 2, :],
@@ -264,22 +279,34 @@ def tile_gcrnncell_pa_kernel(tc, inputs, state, support0, support1, r_kernel, u_
             nc.sync.dma_start(out=u_view[:, :, k, :], in_=ru[:, 1, :, k % 2, :])
 
         def last_block(k):
+            sc, ss = sup_codes[k]
             st = state_of[k]
-            ru = pair_tiles[("ru", k // 2)]
             g2 = hs_pool.tile([P, 1024], BF16, name="g2", tag="g2", align_bytes=64)
             g2c = hs_pool.tile([P, 256], U32, name="g2c", tag="g2c", align_bytes=64)
             g2s = hs_pool.tile([P, 256], U8, name="g2s", tag="g2s", align_bytes=64)
-            ob0 = ps_o.tile([P, 512], F32, name="ob", tag="ob")
-            ob1 = ps_g.tile([P, 512], F32, name="gb", tag="gb")
-            banks = (ob0, ob1)
             for b in range(2):
-                for i in range(2):
-                    nc.tensor.transpose(st["H"][b][:, i * P:(i + 1) * P], st["h32"][:, b, k % 2, i, :], ident[:])
+                for g in range(4):
+                    a = (2 * g + b) * P
+                    nc.tensor.matmul_mx(
+                        out=st["H"][b][:, 256:512],
+                        lhsT=xc[:, 1, a:a + P].bitcast(FP8X4),
+                        lhsT_scale=xs[:, 1, a:a + P],
+                        rhs=sc[:, 256 * g:256 * g + 256].bitcast(FP8X4),
+                        rhs_scale=ss[:, 256 * g:256 * g + 256],
+                        start=(g == 0),
+                        stop=(g == 3),
+                    )
                 copy_on(
                     b,
                     g2[:, 512 * b:512 * b + 512].rearrange("p (m t) -> p m t", t=4),
                     st["H"][b][:].rearrange("p (t m) -> p m t", t=4),
                 )
+            gates(k - 1)
+            store_ru_block(k - 1)
+            ru = pair_tiles[("ru", k // 2)]
+            ob0 = ps_g.tile([P, 512], F32, name="gb", tag="gb")
+            ob1 = ring.tile([P, 512], F32, name="tp", tag="bank")
+            banks = (ob0, ob1)
             for b in range(2):
                 nc.vector.quantize_mx(
                     out=g2c[:, P * b:P * b + P].bitcast(FP8X4),
@@ -307,48 +334,105 @@ def tile_gcrnncell_pa_kernel(tc, inputs, state, support0, support1, r_kernel, u_
                 else:
                     nc.scalar.dma_start(out=u_view[:, b, k, :], in_=ru[:, 1, b, k % 2, :])
 
+        for half in range(2):
+            for b in range(2):
+                load_x_half(b, half)
+        for half in range(2):
+            for i in range(2):
+                load_first_sup_half(i, half)
+        load_sup(1)
+        load_w()
+        load_x(1)
+        for k in range(2, RAW_BUFS):
+            load_sup(k)
+
+        def turn_and_load(k):
+            turn_sup(k)
+            if k + RAW_BUFS - 3 < NBLK and k >= 3:
+                load_sup(k + RAW_BUFS - 3)
+
         keep_clock(6)
         prepare_x(0)
-        keep_clock(3)
-        plain_phase([], [0])
-        keep_clock(1)
+        turn_sup(0)
+        quantise_sup(0)
+        keep_clock(2)
+        turn_sup(1)
+        quantise_sup(1)
+        feats_passes(0)
+        feats_passes(1, ring, "bank")
         prepare_x(1)
-        keep_clock(3)
-
-        wg = const.tile([P, 2, P, 4], BF16, name="wg", tag="wg", align_bytes=64)
-        wc = const.tile([P, 256], U32, name="wc", tag="wc", align_bytes=64)
-        ws = const.tile([P, 256], U8, name="ws", tag="ws", align_bytes=64)
-
-        def mx_block(k, gate_k):
-            feats_passes(k)
-            if gate_k is not None:
-                ob = gate_passes(gate_k)
-                gate_sigmoid(gate_k, ob)
-            prev_passes(k)
-            if k % 2 == 1:
-                store_h(k // 2)
-            if gate_k is not None and gate_k % 2 == 1:
-                store_ru(gate_k // 2)
-
-        plain_phase([], [1])
+        turn_sup(2, (1, 1, 1, 1))
         nc.vector.tensor_copy(out=wg[:], in_=wraw[:].rearrange("p r t u -> p r u t"))
         nc.vector.quantize_mx(out=wc[:].bitcast(FP8X4), scales=ws[:], in_=wg[:].rearrange("p r u t -> p (r u t)"))
-        mx_block(0, None)
-        plain_phase([0], [2])
-        mx_block(1, 0)
-        plain_phase([1], [3, 4])
-        mx_block(2, 1)
-        mx_block(3, None)
-        for a in range(2, NBLK - 4, 2):
-            plain_phase([a, a + 1], [a + 3, a + 4])
-            mx_block(a + 2, a)
-            mx_block(a + 3, a + 1)
-        plain_phase([NBLK - 4, NBLK - 3], [NBLK - 1])
-        mx_block(NBLK - 2, NBLK - 4)
-        ob = gate_passes(NBLK - 3)
-        gate_sigmoid(NBLK - 3, ob)
-        store_ru((NBLK - 3) // 2)
-        plain_phase([NBLK - 2], [])
-        mx_block(NBLK - 1, NBLK - 2)
-        store_ru_block(NBLK - 2)
+        turn_h(0)
+        turn_h(1)
+        store_h(0)
+        prev_passes(0)
+        quantise_sup(2)
+        regroup(0)
+        prev_passes(1)
+        regroup(1)
+        quantise_hs(0)
+        feats_passes(2)
+
+        turn_and_load(3)
+        turn_and_load(4)
+        turn_h(2)
+        quantise_hs(1)
+        quantise_sup(3)
+        gates(0)
+        prev_passes(2)
+        regroup(2)
+        feats_passes(3)
+        store_h(1)
+        gates(1)
+        store_ru(0)
+        quantise_sup(4)
+        quantise_hs(2)
+
+        turn_and_load(5)
+        turn_and_load(6)
+        turn_h(3)
+        quantise_sup(5)
+        feats_passes(4)
+        prev_passes(3)
+        regroup(3)
+        gates(2)
+        quantise_half(6, 0)
+        quantise_hs(3)
+        quantise_half(6, 1)
+        feats_passes(5)
+        store_h(2)
+        gates(3)
+        store_ru(1)
+
+        for a in range(4, NBLK - 2, 2):
+            turn_and_load(a + 3)
+            if a + 4 < NBLK:
+                turn_and_load(a + 4)
+            turn_h(a)
+            turn_h(a + 1)
+            quantise_sup(a + 3)
+            prev_passes(a)
+            regroup(a)
+            feats_passes(a + 2)
+            if a + 4 < NBLK:
+                quantise_half(a + 4, 0)
+            quantise_hs(a)
+            if a + 4 < NBLK:
+                quantise_half(a + 4, 1)
+            prev_passes(a + 1)
+            regroup(a + 1)
+            gates(a)
+            feats_passes(a + 3)
+            store_h((a + 2) // 2)
+            quantise_hs(a + 1)
+            gates(a + 1)
+            store_ru(a // 2)
+
+        turn_h(NBLK - 2)
+        turn_h(NBLK - 1)
+        prev_passes(NBLK - 2)
+        regroup(NBLK - 2)
+        quantise_hs(NBLK - 2)
         last_block(NBLK - 1)

@@ -14,6 +14,7 @@ P = 128
 NODES = 2048
 NBLK = 16
 RAW_BUFS = 9
+XW = 512
 FLOPS = 2 * 2 * 512 * NODES * NODES + 2 * 4096 * 512 * 256
 
 
@@ -55,10 +56,10 @@ def tile_gcrnncell_pa_kernel(tc, inputs, state, support0, support1, r_kernel, u_
         wc = const.tile([P, 256], U32, name="wc", tag="wc", align_bytes=64)
         ws = const.tile([P, 256], U8, name="ws", tag="ws", align_bytes=64)
 
-        def keep_clock(n):
-            tp = ring.tile([P, 512], F32, name="tp", tag="bank")
+        def keep_clock(n, width=512):
+            tp = ps_o.tile([P, 512], F32, name="ob", tag="ob")
             for d in range(n):
-                nc.tensor.matmul(out=tp[:], lhsT=zeros[:, 0:P], rhs=zeros[:], start=True, stop=True)
+                nc.tensor.matmul(out=tp[:, 0:width], lhsT=zeros[:, 0:P], rhs=zeros[:, 0:width], start=True, stop=True)
 
         raw = {}
         xr = {}
@@ -114,6 +115,8 @@ def tile_gcrnncell_pa_kernel(tc, inputs, state, support0, support1, r_kernel, u_
                             col = 256 * gg + 128 * u
                             dst = (2 * gg + u) * P
                             nc.tensor.transpose(tp[:, dst:dst + P], words[:, col:col + P], ident[:])
+                    if kind == 0:
+                        keep_clock(1, XW)
                     copy_on(b, xg32[:, 2 * gp:2 * gp + 2, b, :, :], tp[:].rearrange("p (g u c) -> p g c u", g=2, u=2))
             for half in range(2):
                 nc.vector.quantize_mx(
@@ -126,13 +129,15 @@ def tile_gcrnncell_pa_kernel(tc, inputs, state, support0, support1, r_kernel, u_
         grouped_of = {}
         state_of = {}
 
-        def transpose_bank(k, g, grouped, which):
+        def transpose_bank(k, g, grouped, which, dummy):
             tp = ring.tile([P, 512], F32, name="tp", tag="bank")
             for i in range(2):
                 words = sup_words(k, i, g)
                 for u in range(2):
                     dst = (2 * i + u) * P
                     nc.tensor.transpose(tp[:, dst:dst + P], words[:, 128 * u:128 * u + 128], ident[:])
+                if i == 0 and dummy:
+                    keep_clock(1 if dummy < 513 else 3, min(dummy, 512))
             copy_on(
                 which,
                 grouped[:].bitcast(F32)[:, 512 * g:512 * g + 512].rearrange("p (i m u) -> p i m u", i=2, u=2),
@@ -143,10 +148,10 @@ def tile_gcrnncell_pa_kernel(tc, inputs, state, support0, support1, r_kernel, u_
             gt = grp_pool.tile([P, 4096], BF16, name="grouped", tag="grouped", align_bytes=64)
             grouped_of[k] = gt
 
-        def turn_sup(k, engines=(0, 1, 0, 1)):
+        def turn_sup(k, engines=(0, 1, 0, 1), dummies=(0, 0, 0, 0)):
             new_grouped(k)
             for g in range(4):
-                transpose_bank(k, g, grouped_of[k], engines[g])
+                transpose_bank(k, g, grouped_of[k], engines[g], dummies[g])
 
         def quantise_half(k, half):
             if half == 0:
@@ -341,9 +346,11 @@ def tile_gcrnncell_pa_kernel(tc, inputs, state, support0, support1, r_kernel, u_
             for i in range(2):
                 load_first_sup_half(i, half)
         load_sup(1)
-        load_w()
         load_x(1)
-        for k in range(2, RAW_BUFS):
+        load_sup(2)
+        load_sup(3)
+        load_w()
+        for k in range(4, RAW_BUFS):
             load_sup(k)
 
         def turn_and_load(k):
@@ -353,17 +360,15 @@ def tile_gcrnncell_pa_kernel(tc, inputs, state, support0, support1, r_kernel, u_
 
         keep_clock(6)
         prepare_x(0)
-        turn_sup(0)
+        turn_sup(0, dummies=(512, 512, 512, 512))
         quantise_sup(0)
         keep_clock(2)
-        turn_sup(1)
+        turn_sup(1, dummies=(1024, 0, 0, 0))
         quantise_sup(1)
         feats_passes(0)
         feats_passes(1, ring, "bank")
         prepare_x(1)
         turn_sup(2, (1, 1, 1, 1))
-        nc.vector.tensor_copy(out=wg[:], in_=wraw[:].rearrange("p r t u -> p r u t"))
-        nc.vector.quantize_mx(out=wc[:].bitcast(FP8X4), scales=ws[:], in_=wg[:].rearrange("p r u t -> p (r u t)"))
         turn_h(0)
         turn_h(1)
         store_h(0)
@@ -373,6 +378,8 @@ def tile_gcrnncell_pa_kernel(tc, inputs, state, support0, support1, r_kernel, u_
         prev_passes(1)
         regroup(1)
         quantise_hs(0)
+        nc.vector.tensor_copy(out=wg[:], in_=wraw[:].rearrange("p r t u -> p r u t"))
+        nc.vector.quantize_mx(out=wc[:].bitcast(FP8X4), scales=ws[:], in_=wg[:].rearrange("p r u t -> p (r u t)"))
         feats_passes(2)
 
         turn_and_load(3)

@@ -13,7 +13,7 @@ SIGMOID = mybir.ActivationFunctionType.Sigmoid
 P = 128
 NODES = 2048
 NBLK = 16
-RAW_BUFS = 9
+RAW_BUFS = 8
 XW = 512
 FLOPS = 2 * 2 * 512 * NODES * NODES + 2 * 4096 * 512 * 256
 
@@ -24,10 +24,10 @@ def tile_gcrnncell_pa_kernel(tc, inputs, state, support0, support1, r_kernel, u_
         const = ctx.enter_context(tc.tile_pool(name="const", bufs=1))
         raw_pool = ctx.enter_context(tc.tile_pool(name="raw", bufs=RAW_BUFS))
         half_pool = ctx.enter_context(tc.tile_pool(name="half", bufs=4))
-        grp_pool = ctx.enter_context(tc.tile_pool(name="grp", bufs=4))
-        code_pool = ctx.enter_context(tc.tile_pool(name="code", bufs=6))
+        grp_pool = ctx.enter_context(tc.tile_pool(name="grp", bufs=5))
+        code_pool = ctx.enter_context(tc.tile_pool(name="code", bufs=8))
         hs_pool = ctx.enter_context(tc.tile_pool(name="hs", bufs=4))
-        out_pool = ctx.enter_context(tc.tile_pool(name="outs", bufs=3))
+        out_pool = ctx.enter_context(tc.tile_pool(name="outs", bufs=4))
         ring = ctx.enter_context(tc.psum_pool(name="ring", bufs=6))
         ps_g = ctx.enter_context(tc.psum_pool(name="psg", bufs=1))
         ps_o = ctx.enter_context(tc.psum_pool(name="pso", bufs=1))
@@ -397,8 +397,8 @@ def tile_gcrnncell_pa_kernel(tc, inputs, state, support0, support1, r_kernel, u_
         quantise_sup(4)
         quantise_hs(2)
 
-        turn_and_load(5)
-        turn_and_load(6)
+        for k in (5, 6, 7):
+            turn_and_load(k)
         turn_h(3)
         quantise_sup(5)
         feats_passes(4)
@@ -410,36 +410,51 @@ def tile_gcrnncell_pa_kernel(tc, inputs, state, support0, support1, r_kernel, u_
         quantise_half(6, 1)
         feats_passes(5)
         store_h(2)
+        quantise_sup(7)
         gates(3)
         store_ru(1)
+        feats_passes(6, ring, "bank")
 
-        for a in range(4, NBLK - 2, 2):
-            turn_and_load(a + 3)
-            if a + 4 < NBLK:
-                turn_and_load(a + 4)
-            turn_h(a)
-            turn_h(a + 1)
-            quantise_sup(a + 3)
-            prev_passes(a)
-            regroup(a)
-            feats_passes(a + 2)
-            if a + 4 < NBLK:
-                quantise_half(a + 4, 0)
-            quantise_hs(a)
-            if a + 4 < NBLK:
-                quantise_half(a + 4, 1)
-            prev_passes(a + 1)
-            regroup(a + 1)
-            gates(a)
-            feats_passes(a + 3)
-            store_h((a + 2) // 2)
-            quantise_hs(a + 1)
-            gates(a + 1)
-            store_ru(a // 2)
+        def finish(k):
+            gates(k)
+            if k % 2 == 1:
+                store_ru(k // 2)
 
-        turn_h(NBLK - 2)
-        turn_h(NBLK - 1)
-        prev_passes(NBLK - 2)
-        regroup(NBLK - 2)
-        quantise_hs(NBLK - 2)
-        last_block(NBLK - 1)
+        def bunch(blocks, t_blocks):
+            for k in t_blocks:
+                turn_and_load(k)
+            for k in blocks:
+                turn_h(k)
+            for n, k in enumerate(blocks):
+                if n < len(t_blocks):
+                    quantise_half(t_blocks[n], 0)
+                prev_passes(k)
+                if n == 0 and blocks[0] > 4:
+                    finish(blocks[0] - 1)
+                if n >= 1:
+                    quantise_hs(blocks[n - 1])
+                if n < len(t_blocks):
+                    quantise_half(t_blocks[n], 1)
+                regroup(k)
+                if k + 3 < NBLK:
+                    feats_passes(k + 3)
+                    if k % 2 == 0:
+                        store_h((k + 3) // 2)
+                if n >= 1:
+                    finish(blocks[n - 1])
+            quantise_hs(blocks[-1])
+
+        bunch((4, 5, 6), (8, 9, 10))
+        bunch((7, 8, 9), (11, 12, 13))
+        bunch((10, 11, 12), (14, 15))
+        for k in (13, 14, 15):
+            turn_h(k)
+        prev_passes(13)
+        regroup(13)
+        finish(12)
+        prev_passes(14)
+        quantise_hs(13)
+        regroup(14)
+        finish(13)
+        quantise_hs(14)
+        last_block(15)

from contextlib import ExitStack

import concourse.mybir as mybir
from concourse.masks import make_identity

F32 = mybir.dt.float32
BF16 = mybir.dt.bfloat16
U32 = mybir.dt.uint32
U8 = mybir.dt.uint8
FP8X4 = mybir.dt.float8_e4m3fn_x4
SIGMOID = mybir.ActivationFunctionType.Sigmoid

P = 128
NODES = 2048
NBLK = 16
RAW_BUFS = 8
XW = 512
FLOPS = 2 * 2 * 512 * NODES * NODES + 2 * 4096 * 512 * 256


def tile_gcrnncell_pa_kernel(tc, inputs, state, support0, support1, r_kernel, u_kernel, out_0, out_1, out_2):
    nc = tc.nc
    with ExitStack() as ctx:
        const = ctx.enter_context(tc.tile_pool(name="const", bufs=1))
        raw_pool = ctx.enter_context(tc.tile_pool(name="raw", bufs=RAW_BUFS))
        half_pool = ctx.enter_context(tc.tile_pool(name="half", bufs=4))
        grp_pool = ctx.enter_context(tc.tile_pool(name="grp", bufs=5))
        code_pool = ctx.enter_context(tc.tile_pool(name="code", bufs=8))
        hs_pool = ctx.enter_context(tc.tile_pool(name="hs", bufs=4))
        out_pool = ctx.enter_context(tc.tile_pool(name="outs", bufs=4))
        ring = ctx.enter_context(tc.psum_pool(name="ring", bufs=6))
        ps_g = ctx.enter_context(tc.psum_pool(name="psg", bufs=1))
        ps_o = ctx.enter_context(tc.psum_pool(name="pso", bufs=1))
        ctx.enter_context(tc.manual_schedule())

        sup_view = [s.rearrange("(p t) n -> p t n", t=NBLK) for s in (support0, support1)]
        x_view = [inputs.rearrange("b (c n) -> b c n", n=NODES), state.rearrange("b (c n) -> b c n", n=NODES)]
        r_view = out_0.rearrange("b (p t) u -> p b t u", t=NBLK)
        u_view = out_1.rearrange("b (p t) u -> p b t u", t=NBLK)
        h_view = out_2.rearrange("b (p t) f -> p b t f", t=NBLK)

        ident = const.tile([P, P], F32, name="ident", tag="ident")
        make_identity(nc, ident[:])
        warm_in = const.tile([P, 1], F32, name="warm_in", tag="warm_in")
        warm_out = const.tile([P, 1], F32, name="warm_out", tag="warm_out")
        nc.vector.memset(warm_in[:], 0.0)
        nc.scalar.activation(out=warm_out[:], in_=warm_in[:], func=SIGMOID)

        zeros = const.tile([P, 512], BF16, name="zeros", tag="zeros")
        nc.vector.memset(zeros[:], 0.0)

        xc = const.tile([P, 2, 1024], U32, name="xc", tag="xc", align_bytes=64)
        xs = const.tile([P, 2, 1024], U8, name="xs", tag="xs", align_bytes=64)
        wraw = const.tile([P, 2, 4, P], BF16, name="wraw", tag="wraw")
        wg = const.tile([P, 2, P, 4], BF16, name="wg", tag="wg", align_bytes=64)
        wc = const.tile([P, 256], U32, name="wc", tag="wc", align_bytes=64)
        ws = const.tile([P, 256], U8, name="ws", tag="ws", align_bytes=64)

        def keep_clock(n, width=512):
            tp = ps_o.tile([P, 512], F32, name="ob", tag="ob")
            for d in range(n):
                nc.tensor.matmul(out=tp[:, 0:width], lhsT=zeros[:, 0:P], rhs=zeros[:, 0:width], start=True, stop=True)

        raw = {}
        xr = {}
        first_words = {}

        def load_x(kind):
            for b in range(2):
                t = raw_pool.tile([P, NODES], BF16, name="raw%d" % b, tag="raw%d" % b)
                nc.sync.dma_start(out=t[:], in_=x_view[kind][b])
                for half in range(2):
                    xr[(kind, b, half)] = t[:].bitcast(F32)[:, 512 * half:512 * half + 512]

        def load_x_half(b, half):
            t = half_pool.tile([P, 1024], BF16, name="xhalf", tag="xhalf")
            nc.sync.dma_start(out=t[:], in_=x_view[0][b][:, 1024 * half:1024 * half + 1024])
            xr[(0, b, half)] = t[:].bitcast(F32)

        def load_first_sup_half(i, half):
            t = half_pool.tile([P, 1024], BF16, name="shalf", tag="shalf")
            nc.sync.dma_start(out=t[:], in_=sup_view[i][:, 0, 1024 * half:1024 * half + 1024])
            first_words[(i, half)] = t[:].bitcast(F32)

        def sup_words(k, i, g):
            if k == 0:
                return first_words[(i, g // 2)][:, 256 * (g % 2):256 * (g % 2) + 256]
            return raw[(k, i)][:].bitcast(F32)[:, 256 * g:256 * g + 256]

        def load_w():
            for r, kern in enumerate((r_kernel, u_kernel)):
                nc.sync.dma_start(out=wraw[:, r], in_=kern.rearrange("(t p) u -> p t u", p=P))

        def load_sup(k):
            for i in range(2):
                t = raw_pool.tile([P, NODES], BF16, name="raw%d" % i, tag="raw%d" % i)
                nc.sync.dma_start(out=t[:], in_=sup_view[i][:, k, :])
                raw[(k, i)] = t

        def copy_on(which, out, in_):
            if which == 0:
                nc.vector.tensor_copy(out=out, in_=in_)
            else:
                nc.scalar.copy(out=out, in_=in_)

        def prepare_x(kind):
            xg = grp_pool.tile([P, 4096], BF16, name="grouped", tag="grouped", align_bytes=64)
            xg32 = xg[:].bitcast(F32).rearrange("p (g b c u) -> p g b c u", g=4, b=2, u=2)
            for gp in range(2):
                for b in range(2):
                    words = xr[(kind, b, gp)]
                    tp = ring.tile([P, 512], F32, name="tp", tag="bank")
                    for gg in range(2):
                        for u in range(2):
                            col = 256 * gg + 128 * u
                            dst = (2 * gg + u) * P
                            nc.tensor.transpose(tp[:, dst:dst + P], words[:, col:col + P], ident[:])
                    if kind == 0:
                        keep_clock(1, XW)
                    copy_on(b, xg32[:, 2 * gp:2 * gp + 2, b, :, :], tp[:].rearrange("p (g u c) -> p g c u", g=2, u=2))
            for half in range(2):
                nc.vector.quantize_mx(
                    out=xc[:, kind, 512 * half:512 * half + 512].bitcast(FP8X4),
                    scales=xs[:, kind, 512 * half:512 * half + 512],
                    in_=xg[:, 2048 * half:2048 * half + 2048],
                )

        sup_codes = {}
        grouped_of = {}
        state_of = {}

        def transpose_bank(k, g, grouped, which, dummy):
            tp = ring.tile([P, 512], F32, name="tp", tag="bank")
            for i in range(2):
                words = sup_words(k, i, g)
                for u in range(2):
                    dst = (2 * i + u) * P
                    nc.tensor.transpose(tp[:, dst:dst + P], words[:, 128 * u:128 * u + 128], ident[:])
                if i == 0 and dummy:
                    keep_clock(1 if dummy < 513 else 3, min(dummy, 512))
            copy_on(
                which,
                grouped[:].bitcast(F32)[:, 512 * g:512 * g + 512].rearrange("p (i m u) -> p i m u", i=2, u=2),
                tp[:].rearrange("p (i u m) -> p i m u", i=2, u=2),
            )

        def new_grouped(k):
            gt = grp_pool.tile([P, 4096], BF16, name="grouped", tag="grouped", align_bytes=64)
            grouped_of[k] = gt

        def turn_sup(k, engines=(0, 1, 0, 1), dummies=(0, 0, 0, 0)):
            new_grouped(k)
            for g in range(4):
                transpose_bank(k, g, grouped_of[k], engines[g], dummies[g])

        def quantise_half(k, half):
            if half == 0:
                sc = code_pool.tile([P, 1024], U32, name="sc", tag="sc", align_bytes=64)
                ss = code_pool.tile([P, 1024], U8, name="ss", tag="ss", align_bytes=64)
                sup_codes[k] = (sc, ss)
            sc, ss = sup_codes[k]
            nc.vector.quantize_mx(
                out=sc[:, 512 * half:512 * half + 512].bitcast(FP8X4),
                scales=ss[:, 512 * half:512 * half + 512],
                in_=grouped_of[k][:, 2048 * half:2048 * half + 2048],
            )

        def quantise_sup(k):
            quantise_half(k, 0)
            quantise_half(k, 1)

        def turn_h(k):
            st = state_of[k]
            st["H"] = []
            for b in range(2):
                hb = ring.tile([P, 512], F32, name="hb", tag="bank")
                for i in range(2):
                    nc.tensor.transpose(hb[:, i * P:(i + 1) * P], st["h32"][:, b, k % 2, i, :], ident[:])
                st["H"].append(hb)

        def regroup(k):
            st = state_of[k]
            g2 = hs_pool.tile([P, 1024], BF16, name="g2", tag="g2", align_bytes=64)
            st["g2"] = g2
            for b in range(2):
                copy_on(
                    b,
                    g2[:, 512 * b:512 * b + 512].rearrange("p (m t) -> p m t", t=4),
                    st["H"][b][:].rearrange("p (t m) -> p m t", t=4),
                )

        def quantise_hs(k):
            g2 = state_of[k]["g2"]
            g2c = hs_pool.tile([P, 256], U32, name="g2c", tag="g2c", align_bytes=64)
            g2s = hs_pool.tile([P, 256], U8, name="g2s", tag="g2s", align_bytes=64)
            nc.vector.quantize_mx(out=g2c[:].bitcast(FP8X4), scales=g2s[:], in_=g2[:])
            state_of[k]["g2c"] = g2c
            state_of[k]["g2s"] = g2s

        pair_tiles = {}

        def feats_passes(k, pool=ps_g, tag="gb"):
            sc, ss = sup_codes[k]
            gb = pool.tile([P, 512], F32, name="gb", tag=tag)
            for i in range(2):
                for g in range(4):
                    a = (2 * g + i) * P
                    nc.tensor.matmul_mx(
                        out=gb[:, 256 * i:256 * i + 256],
                        lhsT=sc[:, a:a + P].bitcast(FP8X4),
                        lhsT_scale=ss[:, a:a + P],
                        rhs=xc[:, 0, 256 * g:256 * g + 256].bitcast(FP8X4),
                        rhs_scale=xs[:, 0, 256 * g:256 * g + 256],
                        start=(g == 0),
                        stop=(g == 3),
                    )
            if k % 2 == 0:
                h32 = out_pool.tile([P, 2, 2, 2, P], F32, name="h32", tag="h32")
                pair_tiles[("h", k // 2)] = h32
            h32 = pair_tiles[("h", k // 2)]
            nc.scalar.copy(out=h32[:, :, k % 2, :, :], in_=gb[:].rearrange("p (i b c) -> p b i c", i=2, b=2))
            state_of[k] = {"h32": h32}

        def prev_passes(k):
            sc, ss = sup_codes[k]
            for b in range(2):
                hb = state_of[k]["H"][b]
                for g in range(4):
                    a = (2 * g + b) * P
                    nc.tensor.matmul_mx(
                        out=hb[:, 256:512],
                        lhsT=xc[:, 1, a:a + P].bitcast(FP8X4),
                        lhsT_scale=xs[:, 1, a:a + P],
                        rhs=sc[:, 256 * g:256 * g + 256].bitcast(FP8X4),
                        rhs_scale=ss[:, 256 * g:256 * g + 256],
                        start=(g == 0),
                        stop=(g == 3),
                    )

        def gate_passes(k):
            st = state_of[k]
            ob = ps_o.tile([P, 512], F32, name="ob", tag="ob")
            for b in range(2):
                nc.tensor.matmul_mx(
                    out=ob[:, 256 * b:256 * b + 256],
                    lhsT=st["g2c"][:, P * b:P * b + P].bitcast(FP8X4),
                    lhsT_scale=st["g2s"][:, P * b:P * b + P],
                    rhs=wc[:].bitcast(FP8X4),
                    rhs_scale=ws[:],
                    start=True,
                    stop=True,
                )
            return ob

        def gate_sigmoid(k, ob):
            if k % 2 == 0:
                ru = out_pool.tile([P, 2, 2, 2, P], F32, name="ru", tag="ru")
                pair_tiles[("ru", k // 2)] = ru
            ru = pair_tiles[("ru", k // 2)]
            nc.scalar.activation(
                out=ru[:, :, :, k % 2, :].rearrange("p r b u -> p b r u"),
                in_=ob[:].rearrange("p (b r u) -> p b r u", b=2, r=2),
                func=SIGMOID,
            )

        def gates(k):
            ob = gate_passes(k)
            gate_sigmoid(k, ob)

        def store_h(q):
            nc.sync.dma_start(
                out=h_view[:, :, 2 * q:2 * q + 2, :],
                in_=pair_tiles[("h", q)][:].rearrange("p b t i c -> p b t (i c)"),
            )

        def store_ru(q):
            ru = pair_tiles[("ru", q)]
            nc.sync.dma_start(out=r_view[:, :, 2 * q:2 * q + 2, :], in_=ru[:, 0])
            nc.sync.dma_start(out=u_view[:, :, 2 * q:2 * q + 2, :], in_=ru[:, 1])

        def store_ru_block(k):
            ru = pair_tiles[("ru", k // 2)]
            nc.sync.dma_start(out=r_view[:, :, k, :], in_=ru[:, 0, :, k % 2, :])
            nc.sync.dma_start(out=u_view[:, :, k, :], in_=ru[:, 1, :, k % 2, :])

        def last_block(k):
            sc, ss = sup_codes[k]
            st = state_of[k]
            g2 = hs_pool.tile([P, 1024], BF16, name="g2", tag="g2", align_bytes=64)
            g2c = hs_pool.tile([P, 256], U32, name="g2c", tag="g2c", align_bytes=64)
            g2s = hs_pool.tile([P, 256], U8, name="g2s", tag="g2s", align_bytes=64)
            for b in range(2):
                for g in range(4):
                    a = (2 * g + b) * P
                    nc.tensor.matmul_mx(
                        out=st["H"][b][:, 256:512],
                        lhsT=xc[:, 1, a:a + P].bitcast(FP8X4),
                        lhsT_scale=xs[:, 1, a:a + P],
                        rhs=sc[:, 256 * g:256 * g + 256].bitcast(FP8X4),
                        rhs_scale=ss[:, 256 * g:256 * g + 256],
                        start=(g == 0),
                        stop=(g == 3),
                    )
                copy_on(
                    b,
                    g2[:, 512 * b:512 * b + 512].rearrange("p (m t) -> p m t", t=4),
                    st["H"][b][:].rearrange("p (t m) -> p m t", t=4),
                )
            gates(k - 1)
            store_ru_block(k - 1)
            ru = pair_tiles[("ru", k // 2)]
            ob0 = ps_g.tile([P, 512], F32, name="gb", tag="gb")
            ob1 = ring.tile([P, 512], F32, name="tp", tag="bank")
            banks = (ob0, ob1)
            for b in range(2):
                nc.vector.quantize_mx(
                    out=g2c[:, P * b:P * b + P].bitcast(FP8X4),
                    scales=g2s[:, P * b:P * b + P],
                    in_=g2[:, 512 * b:512 * b + 512],
                )
            for b in range(2):
                nc.tensor.matmul_mx(
                    out=banks[b][:, 0:256],
                    lhsT=g2c[:, P * b:P * b + P].bitcast(FP8X4),
                    lhsT_scale=g2s[:, P * b:P * b + P],
                    rhs=wc[:].bitcast(FP8X4),
                    rhs_scale=ws[:],
                    start=True,
                    stop=True,
                )
                nc.scalar.activation(
                    out=ru[:, :, b, k % 2, :],
                    in_=banks[b][:, 0:256].rearrange("p (r u) -> p r u", r=2),
                    func=SIGMOID,
                )
                nc.sync.dma_start(out=r_view[:, b, k, :], in_=ru[:, 0, b, k % 2, :])
                if b == 0:
                    nc.sync.dma_start(out=u_view[:, b, k, :], in_=ru[:, 1, b, k % 2, :])
                else:
                    nc.scalar.dma_start(out=u_view[:, b, k, :], in_=ru[:, 1, b, k % 2, :])

        for half in range(2):
            for b in range(2):
                load_x_half(b, half)
        for half in range(2):
            for i in range(2):
                load_first_sup_half(i, half)
        load_sup(1)
        load_x(1)
        load_sup(2)
        load_sup(3)
        load_w()
        for k in range(4, RAW_BUFS):
            load_sup(k)

        def turn_and_load(k):
            turn_sup(k)
            if k + RAW_BUFS - 3 < NBLK and k >= 3:
                load_sup(k + RAW_BUFS - 3)

        keep_clock(6)
        prepare_x(0)
        turn_sup(0, dummies=(512, 512, 512, 512))
        quantise_sup(0)
        keep_clock(2)
        turn_sup(1, dummies=(1024, 0, 0, 0))
        quantise_sup(1)
        feats_passes(0)
        feats_passes(1, ring, "bank")
        prepare_x(1)
        turn_sup(2, (1, 1, 1, 1))
        turn_h(0)
        turn_h(1)
        store_h(0)
        prev_passes(0)
        quantise_sup(2)
        regroup(0)
        prev_passes(1)
        regroup(1)
        quantise_hs(0)
        nc.vector.tensor_copy(out=wg[:], in_=wraw[:].rearrange("p r t u -> p r u t"))
        nc.vector.quantize_mx(out=wc[:].bitcast(FP8X4), scales=ws[:], in_=wg[:].rearrange("p r u t -> p (r u t)"))
        feats_passes(2)

        turn_and_load(3)
        turn_and_load(4)
        turn_h(2)
        quantise_hs(1)
        quantise_sup(3)
        gates(0)
        prev_passes(2)
        regroup(2)
        feats_passes(3)
        store_h(1)
        gates(1)
        store_ru(0)
        quantise_sup(4)
        quantise_hs(2)

        for k in (5, 6, 7):
            turn_and_load(k)
        turn_h(3)
        quantise_sup(5)
        feats_passes(4)
        prev_passes(3)
        regroup(3)
        gates(2)
        quantise_half(6, 0)
        quantise_hs(3)
        quantise_half(6, 1)
        feats_passes(5)
        store_h(2)
        quantise_sup(7)
        gates(3)
        store_ru(1)
        feats_passes(6, ring, "bank")

        def finish(k):
            gates(k)
            if k % 2 == 1:
                store_ru(k // 2)

        def bunch(blocks, t_blocks):
            for k in t_blocks:
                turn_and_load(k)
            for k in blocks:
                turn_h(k)
            for n, k in enumerate(blocks):
                if n < len(t_blocks):
                    quantise_half(t_blocks[n], 0)
                prev_passes(k)
                if n == 0 and blocks[0] > 4:
                    finish(blocks[0] - 1)
                if n >= 1:
                    quantise_hs(blocks[n - 1])
                if n < len(t_blocks):
                    quantise_half(t_blocks[n], 1)
                regroup(k)
                if k + 3 < NBLK:
                    feats_passes(k + 3)
                    if k % 2 == 0:
                        store_h((k + 3) // 2)
                if n >= 1:
                    finish(blocks[n - 1])
            quantise_hs(blocks[-1])

        bunch((4, 5, 6), (8, 9, 10))
        bunch((7, 8, 9), (11, 12, 13))
        bunch((10, 11, 12), (14, 15))
        for k in (13, 14, 15):
            turn_h(k)
        prev_passes(13)
        regroup(13)
        finish(12)
        prev_passes(14)
        quantise_hs(13)
        regroup(14)
        finish(13)
        quantise_hs(14)
        last_block(15)
